import numpy as np
import ml_dtypes


def mxq(x, axis, fmt="e4m3"):
    dtype, down = {"e4m3": (ml_dtypes.float8_e4m3fn, 7), "e5m2": (ml_dtypes.float8_e5m2, 14)}[fmt]
    v = np.moveaxis(np.asarray(x, np.float32).astype(ml_dtypes.bfloat16).astype(np.float64), axis, -1)
    blocks = v.reshape(v.shape[:-1] + (-1, 32))
    amax = np.abs(blocks).max(-1, keepdims=True)
    byte = np.maximum(np.where(amax > 0, np.frexp(amax)[1] - 1 + 127, 0) - down, 1)
    scale = np.exp2(byte - 127.0)
    codes = (blocks / scale).astype(np.float32).astype(dtype).astype(np.float64)
    return np.moveaxis((codes * scale).reshape(v.shape), -1, axis)


WIDE = False


def mx_kscale(k):
    if not WIDE:
        return np.ones(k)
    levels = np.array([10, -10, 5, -5, 0])
    a = np.random.permutation(np.resize(levels, k // 512 * 4)).reshape(k // 512, 4)
    idx = np.arange(k)
    return np.exp2(a[idx // 512, idx % 128 // 32])


BF16 = ml_dtypes.bfloat16


def bf(x):
    return np.asarray(x, np.float32).astype(BF16)


def f64(x):
    return np.asarray(x).astype(np.float64)


N, D, K, H = 65536, 64, 8, 256


def setup_inputs():
    s = mx_kscale(N)
    t = s / s.min()
    lg = np.random.standard_normal((N, K)) * 1.5
    g = np.exp(lg - lg.max(1, keepdims=True))
    g = g / g.sum(1, keepdims=True)
    return {"z_batch": bf(np.random.standard_normal((N, D)) * t[:, None]),
            "gamma": bf(g / (t * t)[:, None]),
            "mu": bf(np.random.standard_normal((K, D)) * 0.1),
            "gamma_mass": bf(N / K * np.random.uniform(0.6, 1.4, K))}


def reference(z_batch, gamma, mu, gamma_mass):
    zc = f64(z_batch)[None, :, :] - f64(mu)[:, None, :]
    gz = f64(gamma).T[:, :, None] * zc
    sc = mxq(gz, 1, "e4m3").transpose(0, 2, 1) @ mxq(zc, 1, "e4m3")
    return sc / f64(gamma_mass)[:, None, None]

@@ -1,0 +1,236 @@
+from contextlib import ExitStack
+
+import concourse.mybir as mybir
+from concourse.masks import make_identity
+
+F32 = mybir.dt.float32
+BF16 = mybir.dt.bfloat16
+U32 = mybir.dt.uint32
+U8 = mybir.dt.uint8
+FP8X4 = mybir.dt.float8_e4m3fn_x4
+ALU = mybir.AluOpType
+ACTF = mybir.ActivationFunctionType
+
+N, D, K = 65536, 64, 8
+P = 128
+PACK = 4
+K_PASS = P * PACK
+PASSES = N // K_PASS
+GROUP = 4
+GROUPS = PASSES // GROUP
+PAIRS = K // 2
+BLOCKS = 2 * GROUP
+WIDTH = 2 * D * PACK
+CHUNK = 16
+ZBUFS = 4
+BANKS = 6
+ACT_BLOCKS = 3
+PIN = False
+
+FLOPS = 2 * K * N * D * D
+
+
+def tile_gmmestimationnetwork_pa_kernel(tc, z_batch, gamma, mu, gamma_mass, out):
+    nc = tc.nc
+    with ExitStack() as ctx:
+        const = ctx.enter_context(tc.tile_pool(name="const", bufs=1))
+        stage = ctx.enter_context(tc.tile_pool(name="stage", bufs=ZBUFS))
+        work = ctx.enter_context(tc.tile_pool(name="work", bufs=3))
+        ps_t = ctx.enter_context(tc.psum_pool(name="ps_t", bufs=1))
+        ps_z = ctx.enter_context(tc.psum_pool(name="ps_z", bufs=BANKS))
+        ps_acc = ctx.enter_context(tc.psum_pool(name="ps_acc", bufs=1))
+
+        chunks = {}
+
+        def load_z(ch):
+            zs = stage.tile([P, CHUNK, PACK * D], BF16, name="zs")
+            rows = z_batch[ch * CHUNK * K_PASS : (ch + 1) * CHUNK * K_PASS, :]
+            nc.sync.dma_start(out=zs[:], in_=rows.rearrange("(g p j) d -> p g (j d)", p=P, j=PACK))
+            chunks[ch] = zs
+
+        load_z(0)
+
+        ident_bf = const.tile([P, P], BF16)
+        make_identity(nc, ident_bf[:])
+        ident_f = const.tile([P, P], F32)
+        make_identity(nc, ident_f[:])
+
+        mu_rows = const.tile([P, P], BF16)
+        nc.vector.memset(mu_rows[:], 0.0)
+        nc.scalar.dma_start(out=mu_rows[0:K, 0:D], in_=mu)
+        nc.scalar.dma_start(out=mu_rows[0:K, D : 2 * D], in_=mu)
+        mass_bf = const.tile([P, K], BF16)
+        nc.scalar.dma_start(out=mass_bf[:], in_=gamma_mass.partition_broadcast(P))
+
+        gam_nat = const.tile([P, PASSES, PACK, K], BF16)
+        gam = const.tile([P, PASSES, K, PACK], BF16)
+        QG = PASSES // 4
+        for s in range(4):
+            rows = gamma[s * QG * K_PASS : (s + 1) * QG * K_PASS, :]
+            nc.scalar.dma_start(
+                out=gam_nat[:, s * QG : (s + 1) * QG, :, :].rearrange("p g j c -> p g (j c)"),
+                in_=rows.rearrange("(g p j) c -> p g (j c)", p=P, j=PACK),
+            )
+        for ch in range(1, ZBUFS):
+            load_z(ch)
+
+        mu_ps = ps_t.tile([P, P], BF16, tag="zt")
+        nc.tensor.transpose(mu_ps[:], mu_rows[:], ident_bf[:])
+        neg_mu = const.tile([P, K], F32)
+        nc.vector.tensor_scalar_mul(out=neg_mu[:], in0=mu_ps[:, 0:K], scalar1=-1.0)
+        mass_f = const.tile([P, K], F32)
+        nc.vector.tensor_copy(out=mass_f[:], in_=mass_bf[:])
+        inv_mass = const.tile([P, K], F32)
+        nc.vector.reciprocal(out=inv_mass[:], in_=mass_f[:])
+        for s in range(4):
+            nc.vector.tensor_copy(
+                out=gam[:, s * QG : (s + 1) * QG, :, :],
+                in_=gam_nat[:, s * QG : (s + 1) * QG, :, :].rearrange("p g j c -> p g c j"),
+            )
+
+        zT = const.tile([P, PASSES * 2, P], BF16)
+        acc = ps_acc.tile([P, PAIRS, P], F32)
+
+        zt_banks = {}
+        centred = {}
+        banks = {}
+        qins = {}
+        quantised = {}
+
+        def zt_transposes(gg):
+            zs = chunks[(gg * GROUP) // CHUNK]
+            zt_ps = ps_t.tile([P, BLOCKS, P], BF16, tag="zt")
+            for b in range(BLOCKS):
+                gl = (gg * GROUP + b // 2) % CHUNK
+                jj = b % 2
+                nc.tensor.transpose(zt_ps[:, b, :], zs[:, gl, jj * P : (jj + 1) * P], ident_bf[:])
+            zt_banks[gg] = zt_ps
+
+        def zt_evacuate(gg):
+            nc.scalar.copy(out=zT[:, gg * BLOCKS : (gg + 1) * BLOCKS, :], in_=zt_banks[gg][:])
+            nxt = (gg * GROUP) // CHUNK + ZBUFS
+            if (gg * GROUP) % CHUNK == CHUNK - GROUP and nxt < PASSES // CHUNK:
+                load_z(nxt)
+
+        def centre(k):
+            q, gg = divmod(k, GROUPS)
+            zcT = work.tile([P, 2, BLOCKS, P], F32, name="zcT")
+            b0 = gg * BLOCKS
+            nc.scalar.activation(
+                out=zcT[:, 0, :, :], in_=zT[:, b0 : b0 + BLOCKS, :], func=ACTF.Identity,
+                bias=neg_mu[:, 2 * q : 2 * q + 1], scale=1.0,
+            )
+            nc.scalar.activation(
+                out=zcT[:, 1, 0:ACT_BLOCKS, :], in_=zT[:, b0 : b0 + ACT_BLOCKS, :], func=ACTF.Identity,
+                bias=neg_mu[:, 2 * q + 1 : 2 * q + 2], scale=1.0,
+            )
+            nc.vector.tensor_scalar_add(
+                out=zcT[:, 1, ACT_BLOCKS:BLOCKS, :], in0=zT[:, b0 + ACT_BLOCKS : b0 + BLOCKS, :],
+                scalar1=neg_mu[:, 2 * q + 1 : 2 * q + 2],
+            )
+            centred[k] = zcT
+
+        def fill(k, g4):
+            zcT = centred[k]
+            bank = ps_z.tile([P, 2, PACK, D], F32, name="bank")
+            for c2 in range(2):
+                for jj in range(2):
+                    nc.tensor.transpose(
+                        bank[:, c2, 2 * jj : 2 * jj + 2, :].rearrange("p a d -> p (a d)"),
+                        zcT[:, c2, 2 * g4 + jj, :],
+                        ident_f[:],
+                    )
+            banks[(k, g4)] = bank
+
+        def drain_zc(k, g4):
+            nc.scalar.copy(
+                out=qins[k][:, 0, g4, :].rearrange("p (c d j) -> p c d j", c=2, j=PACK),
+                in_=banks[(k, g4)][:].rearrange("p c j d -> p c d j"),
+            )
+
+        def drain_gz(k, g4):
+            q, gg = divmod(k, GROUPS)
+            g = gg * GROUP + g4
+            nc.vector.tensor_tensor(
+                out=qins[k][:, 1, g4, :].rearrange("p (c d j) -> p c d j", c=2, j=PACK),
+                in0=banks[(k, g4)][:].rearrange("p c j d -> p c d j"),
+                in1=gam[:, g, 2 * q : 2 * q + 2, :].unsqueeze(2).to_broadcast([P, 2, D, PACK]),
+                op=ALU.mult,
+            )
+
+        def quantise(k):
+            codes = work.tile([P, 2 * GROUP * P], U32, name="codes", align_bytes=64)
+            scales = work.tile([P, 2 * GROUP * P], U8, name="scales", align_bytes=64)
+            nc.vector.quantize_mx(
+                out=codes[:].bitcast(FP8X4), scales=scales[:],
+                in_=qins[k][:].rearrange("p a g w -> p (a g w)"),
+            )
+            quantised[k] = (codes, scales)
+
+        def multiply(k):
+            q, gg = divmod(k, GROUPS)
+            codes, scales = quantised[k]
+            for g4 in range(GROUP):
+                g = gg * GROUP + g4
+                zc_cols = slice(g4 * P, (g4 + 1) * P)
+                gz_cols = slice((GROUP + g4) * P, (GROUP + g4 + 1) * P)
+                nc.tensor.matmul_mx(
+                    out=acc[:, q, :],
+                    lhsT=codes[:, gz_cols].bitcast(FP8X4), lhsT_scale=scales[:, gz_cols],
+                    rhs=codes[:, zc_cols].bitcast(FP8X4), rhs_scale=scales[:, zc_cols],
+                    start=(g == 0), stop=(g == PASSES - 1),
+                )
+
+        TOTAL = PAIRS * GROUPS
+
+        def body():
+            for gg in range(3):
+                zt_transposes(gg)
+                zt_evacuate(gg)
+            centre(0)
+            centre(1)
+            for g4 in range(GROUP):
+                fill(0, g4)
+            for i in range(TOTAL):
+                if i >= 1:
+                    multiply(i - 1)
+                if i + 3 < GROUPS:
+                    zt_transposes(i + 3)
+                qins[i] = work.tile([P, 2, GROUP, WIDTH], BF16, name="qin", align_bytes=64)
+                if i + 1 < TOTAL:
+                    fill(i + 1, 0)
+                    fill(i + 1, 1)
+                drain_zc(i, 0)
+                drain_gz(i, 1)
+                drain_gz(i, 0)
+                drain_zc(i, 1)
+                if i + 1 < TOTAL:
+                    fill(i + 1, 2)
+                    fill(i + 1, 3)
+                drain_zc(i, 2)
+                drain_gz(i, 3)
+                drain_gz(i, 2)
+                drain_zc(i, 3)
+                if i + 3 < GROUPS:
+                    zt_evacuate(i + 3)
+                if i + 2 < TOTAL:
+                    centre(i + 2)
+                quantise(i)
+            multiply(TOTAL - 1)
+
+        if PIN:
+            with tc.manual_schedule():
+                body()
+        else:
+            body()
+
+        res = const.tile([P, PAIRS, D], F32)
+        for c2 in range(2):
+            rows = slice(c2 * D, (c2 + 1) * D)
+            nc.vector.tensor_tensor(
+                out=res[rows, :, :],
+                in0=acc[rows, :, c2 * D : (c2 + 1) * D],
+                in1=inv_mass[rows, :].rearrange("p (q c) -> p q c", c=2)[:, :, c2 : c2 + 1].to_broadcast([D, PAIRS, D]),
+                op=ALU.mult,
+            )
+        nc.sync.dma_start(out=out.rearrange("(q c) i j -> (c i) q j", c=2), in_=res[:])

@@ -25,7 +25,7 @@ CHUNK = 16
 ZBUFS = 4
 BANKS = 6
 ACT_BLOCKS = 3
-PIN = False
+PIN = True
 
 FLOPS = 2 * K * N * D * D
 
@@ -112,9 +112,19 @@ def tile_gmmestimationnetwork_pa_kernel(tc, z_batch, gamma, mu, gamma_mass, out)
             if (gg * GROUP) % CHUNK == CHUNK - GROUP and nxt < PASSES // CHUNK:
                 load_z(nxt)
 
-        def centre(k):
+        def centre_vector(k):
             q, gg = divmod(k, GROUPS)
             zcT = work.tile([P, 2, BLOCKS, P], F32, name="zcT")
+            centred[k] = zcT
+            b0 = gg * BLOCKS
+            nc.vector.tensor_scalar_add(
+                out=zcT[:, 1, ACT_BLOCKS:BLOCKS, :], in0=zT[:, b0 + ACT_BLOCKS : b0 + BLOCKS, :],
+                scalar1=neg_mu[:, 2 * q + 1 : 2 * q + 2],
+            )
+
+        def centre_scalar(k):
+            q, gg = divmod(k, GROUPS)
+            zcT = centred[k]
             b0 = gg * BLOCKS
             nc.scalar.activation(
                 out=zcT[:, 0, :, :], in_=zT[:, b0 : b0 + BLOCKS, :], func=ACTF.Identity,
@@ -124,11 +134,6 @@ def tile_gmmestimationnetwork_pa_kernel(tc, z_batch, gamma, mu, gamma_mass, out)
                 out=zcT[:, 1, 0:ACT_BLOCKS, :], in_=zT[:, b0 : b0 + ACT_BLOCKS, :], func=ACTF.Identity,
                 bias=neg_mu[:, 2 * q + 1 : 2 * q + 2], scale=1.0,
             )
-            nc.vector.tensor_scalar_add(
-                out=zcT[:, 1, ACT_BLOCKS:BLOCKS, :], in0=zT[:, b0 + ACT_BLOCKS : b0 + BLOCKS, :],
-                scalar1=neg_mu[:, 2 * q + 1 : 2 * q + 2],
-            )
-            centred[k] = zcT
 
         def fill(k, g4):
             zcT = centred[k]
@@ -182,41 +187,57 @@ def tile_gmmestimationnetwork_pa_kernel(tc, z_batch, gamma, mu, gamma_mass, out)
                 )
 
         TOTAL = PAIRS * GROUPS
+        UNITS = TOTAL * GROUP
+
+        def fill_u(u):
+            if 0 <= u < UNITS:
+                fill(u // GROUP, u % GROUP)
+
+        def zc_u(u):
+            if u % GROUP == 0:
+                qins[u // GROUP] = work.tile([P, 2, GROUP, WIDTH], BF16, name="qin", align_bytes=64)
+            drain_zc(u // GROUP, u % GROUP)
+
+        def gz_u(u):
+            if 0 <= u < UNITS:
+                drain_gz(u // GROUP, u % GROUP)
 
         def body():
             for gg in range(3):
                 zt_transposes(gg)
                 zt_evacuate(gg)
-            centre(0)
-            centre(1)
-            for g4 in range(GROUP):
-                fill(0, g4)
-            for i in range(TOTAL):
-                if i >= 1:
-                    multiply(i - 1)
+            for k in range(2):
+                centre_vector(k)
+                centre_scalar(k)
+            for u in range(GROUP):
+                fill_u(u)
+            for i in range(TOTAL + 1):
+                u0 = GROUP * i
+                gz_u(u0 - 2)
+                fill_u(u0 + 4)
+                gz_u(u0 - 1)
+                fill_u(u0 + 5)
                 if i + 3 < GROUPS:
                     zt_transposes(i + 3)
-                qins[i] = work.tile([P, 2, GROUP, WIDTH], BF16, name="qin", align_bytes=64)
-                if i + 1 < TOTAL:
-                    fill(i + 1, 0)
-                    fill(i + 1, 1)
-                drain_zc(i, 0)
-                drain_gz(i, 1)
-                drain_gz(i, 0)
-                drain_zc(i, 1)
-                if i + 1 < TOTAL:
-                    fill(i + 1, 2)
-                    fill(i + 1, 3)
-                drain_zc(i, 2)
-                drain_gz(i, 3)
-                drain_gz(i, 2)
-                drain_zc(i, 3)
+                if i >= 1:
+                    quantise(i - 1)
+                    multiply(i - 1)
+                if i == TOTAL:
+                    break
+                zc_u(u0)
+                zc_u(u0 + 1)
+                if i + 2 < TOTAL:
+                    centre_vector(i + 2)
+                gz_u(u0)
+                fill_u(u0 + 6)
+                gz_u(u0 + 1)
+                fill_u(u0 + 7)
+                zc_u(u0 + 2)
+                zc_u(u0 + 3)
+                if i + 2 < TOTAL:
+                    centre_scalar(i + 2)
                 if i + 3 < GROUPS:
                     zt_evacuate(i + 3)
-                if i + 2 < TOTAL:
-                    centre(i + 2)
-                quantise(i)
-            multiply(TOTAL - 1)
 
         if PIN:
             with tc.manual_schedule():

@@ -21,10 +21,10 @@ GROUPS = PASSES // GROUP
 PAIRS = K // 2
 BLOCKS = 2 * GROUP
 WIDTH = 2 * D * PACK
-CHUNK = 16
+CHUNK = 8
 ZBUFS = 4
 BANKS = 6
-ACT_BLOCKS = 3
+EVAC_ACT = 4
 PIN = True
 
 FLOPS = 2 * K * N * D * D
@@ -88,7 +88,9 @@ def tile_gmmestimationnetwork_pa_kernel(tc, z_batch, gamma, mu, gamma_mass, out)
                 in_=gam_nat[:, s * QG : (s + 1) * QG, :, :].rearrange("p g j c -> p g c j"),
             )
 
-        zT = const.tile([P, PASSES * 2, P], BF16)
+        zT = const.tile([P, PASSES * 2, P], F32)
+        neg_mu_wide = const.tile([P, K, P], F32)
+        nc.vector.tensor_copy(out=neg_mu_wide[:], in_=neg_mu[:].unsqueeze(2).to_broadcast([P, K, P]))
         acc = ps_acc.tile([P, PAIRS, P], F32)
 
         zt_banks = {}
@@ -106,45 +108,47 @@ def tile_gmmestimationnetwork_pa_kernel(tc, z_batch, gamma, mu, gamma_mass, out)
                 nc.tensor.transpose(zt_ps[:, b, :], zs[:, gl, jj * P : (jj + 1) * P], ident_bf[:])
             zt_banks[gg] = zt_ps
 
-        def zt_evacuate(gg):
-            nc.scalar.copy(out=zT[:, gg * BLOCKS : (gg + 1) * BLOCKS, :], in_=zt_banks[gg][:])
+        def zt_evacuate_vector(gg):
+            b0 = gg * BLOCKS
+            nc.vector.tensor_copy(out=zT[:, b0 + EVAC_ACT : b0 + BLOCKS, :], in_=zt_banks[gg][:, EVAC_ACT:BLOCKS, :])
+
+        def zt_evacuate_scalar(gg):
+            b0 = gg * BLOCKS
+            nc.scalar.copy(out=zT[:, b0 : b0 + EVAC_ACT, :], in_=zt_banks[gg][:, 0:EVAC_ACT, :])
             nxt = (gg * GROUP) // CHUNK + ZBUFS
             if (gg * GROUP) % CHUNK == CHUNK - GROUP and nxt < PASSES // CHUNK:
                 load_z(nxt)
 
-        def centre_vector(k):
-            q, gg = divmod(k, GROUPS)
-            zcT = work.tile([P, 2, BLOCKS, P], F32, name="zcT")
-            centred[k] = zcT
-            b0 = gg * BLOCKS
-            nc.vector.tensor_scalar_add(
-                out=zcT[:, 1, ACT_BLOCKS:BLOCKS, :], in0=zT[:, b0 + ACT_BLOCKS : b0 + BLOCKS, :],
-                scalar1=neg_mu[:, 2 * q + 1 : 2 * q + 2],
-            )
-
         def centre_scalar(k):
             q, gg = divmod(k, GROUPS)
-            zcT = centred[k]
+            zcT = work.tile([P, BLOCKS, P], F32, name="zcT")
+            centred[k] = zcT
             b0 = gg * BLOCKS
             nc.scalar.activation(
-                out=zcT[:, 0, :, :], in_=zT[:, b0 : b0 + BLOCKS, :], func=ACTF.Identity,
+                out=zcT[:], in_=zT[:, b0 : b0 + BLOCKS, :], func=ACTF.Identity,
                 bias=neg_mu[:, 2 * q : 2 * q + 1], scale=1.0,
-            )
-            nc.scalar.activation(
-                out=zcT[:, 1, 0:ACT_BLOCKS, :], in_=zT[:, b0 : b0 + ACT_BLOCKS, :], func=ACTF.Identity,
-                bias=neg_mu[:, 2 * q + 1 : 2 * q + 2], scale=1.0,
             )
 
         def fill(k, g4):
+            q, gg = divmod(k, GROUPS)
             zcT = centred[k]
             bank = ps_z.tile([P, 2, PACK, D], F32, name="bank")
-            for c2 in range(2):
-                for jj in range(2):
-                    nc.tensor.transpose(
-                        bank[:, c2, 2 * jj : 2 * jj + 2, :].rearrange("p a d -> p (a d)"),
-                        zcT[:, c2, 2 * g4 + jj, :],
-                        ident_f[:],
-                    )
+            for jj in range(2):
+                nc.tensor.transpose(
+                    bank[:, 0, 2 * jj : 2 * jj + 2, :].rearrange("p a d -> p (a d)"),
+                    zcT[:, 2 * g4 + jj, :],
+                    ident_f[:],
+                )
+            for jj in range(2):
+                region = bank[:, 1, 2 * jj : 2 * jj + 2, :].rearrange("p a d -> p (a d)")
+                nc.tensor.matmul(
+                    out=region, lhsT=neg_mu_wide[:, 2 * q + 1, :], rhs=ident_f[:],
+                    is_transpose=True, start=True, stop=False,
+                )
+                nc.tensor.matmul(
+                    out=region, lhsT=zT[:, gg * BLOCKS + 2 * g4 + jj, :], rhs=ident_f[:],
+                    is_transpose=True, start=False, stop=True,
+                )
             banks[(k, g4)] = bank
 
         def drain_zc(k, g4):
@@ -205,39 +209,40 @@ def tile_gmmestimationnetwork_pa_kernel(tc, z_batch, gamma, mu, gamma_mass, out)
         def body():
             for gg in range(3):
                 zt_transposes(gg)
-                zt_evacuate(gg)
+                zt_evacuate_vector(gg)
+                zt_evacuate_scalar(gg)
             for k in range(2):
-                centre_vector(k)
                 centre_scalar(k)
             for u in range(GROUP):
                 fill_u(u)
             for i in range(TOTAL + 1):
                 u0 = GROUP * i
+                live = i < TOTAL
                 gz_u(u0 - 2)
                 fill_u(u0 + 4)
                 gz_u(u0 - 1)
                 fill_u(u0 + 5)
+                if live:
+                    zc_u(u0)
+                    gz_u(u0)
+                    fill_u(u0 + 6)
                 if i + 3 < GROUPS:
                     zt_transposes(i + 3)
                 if i >= 1:
                     quantise(i - 1)
                     multiply(i - 1)
-                if i == TOTAL:
-                    break
-                zc_u(u0)
-                zc_u(u0 + 1)
-                if i + 2 < TOTAL:
-                    centre_vector(i + 2)
-                gz_u(u0)
-                fill_u(u0 + 6)
-                gz_u(u0 + 1)
-                fill_u(u0 + 7)
-                zc_u(u0 + 2)
-                zc_u(u0 + 3)
-                if i + 2 < TOTAL:
-                    centre_scalar(i + 2)
-                if i + 3 < GROUPS:
-                    zt_evacuate(i + 3)
+                if live:
+                    zc_u(u0 + 1)
+                    if i + 3 < GROUPS:
+                        zt_evacuate_vector(i + 3)
+                    gz_u(u0 + 1)
+                    fill_u(u0 + 7)
+                    zc_u(u0 + 2)
+                    zc_u(u0 + 3)
+                    if i + 2 < TOTAL:
+                        centre_scalar(i + 2)
+                    if i + 3 < GROUPS:
+                        zt_evacuate_scalar(i + 3)
 
         if PIN:
             with tc.manual_schedule():

@@ -21,11 +21,12 @@ GROUPS = PASSES // GROUP
 PAIRS = K // 2
 BLOCKS = 2 * GROUP
 WIDTH = 2 * D * PACK
-CHUNK = 8
+CHUNK = 16
 ZBUFS = 4
 BANKS = 6
-EVAC_ACT = 4
+ACT_BLOCKS = 3
 PIN = True
+MX_N = 512
 
 FLOPS = 2 * K * N * D * D
 
@@ -88,10 +89,9 @@ def tile_gmmestimationnetwork_pa_kernel(tc, z_batch, gamma, mu, gamma_mass, out)
                 in_=gam_nat[:, s * QG : (s + 1) * QG, :, :].rearrange("p g j c -> p g c j"),
             )
 
-        zT = const.tile([P, PASSES * 2, P], F32)
-        neg_mu_wide = const.tile([P, K, P], F32)
-        nc.vector.tensor_copy(out=neg_mu_wide[:], in_=neg_mu[:].unsqueeze(2).to_broadcast([P, K, P]))
-        acc = ps_acc.tile([P, PAIRS, P], F32)
+        zT = const.tile([P, PASSES * 2, P], BF16)
+        res = const.tile([P, PAIRS, D], F32)
+        accs = {}
 
         zt_banks = {}
         centred = {}
@@ -108,47 +108,45 @@ def tile_gmmestimationnetwork_pa_kernel(tc, z_batch, gamma, mu, gamma_mass, out)
                 nc.tensor.transpose(zt_ps[:, b, :], zs[:, gl, jj * P : (jj + 1) * P], ident_bf[:])
             zt_banks[gg] = zt_ps
 
-        def zt_evacuate_vector(gg):
-            b0 = gg * BLOCKS
-            nc.vector.tensor_copy(out=zT[:, b0 + EVAC_ACT : b0 + BLOCKS, :], in_=zt_banks[gg][:, EVAC_ACT:BLOCKS, :])
-
-        def zt_evacuate_scalar(gg):
-            b0 = gg * BLOCKS
-            nc.scalar.copy(out=zT[:, b0 : b0 + EVAC_ACT, :], in_=zt_banks[gg][:, 0:EVAC_ACT, :])
+        def zt_evacuate(gg):
+            nc.scalar.copy(out=zT[:, gg * BLOCKS : (gg + 1) * BLOCKS, :], in_=zt_banks[gg][:])
             nxt = (gg * GROUP) // CHUNK + ZBUFS
             if (gg * GROUP) % CHUNK == CHUNK - GROUP and nxt < PASSES // CHUNK:
                 load_z(nxt)
 
-        def centre_scalar(k):
+        def centre_vector(k):
             q, gg = divmod(k, GROUPS)
-            zcT = work.tile([P, BLOCKS, P], F32, name="zcT")
+            zcT = work.tile([P, 2, BLOCKS, P], F32, name="zcT")
             centred[k] = zcT
             b0 = gg * BLOCKS
+            nc.vector.tensor_scalar_add(
+                out=zcT[:, 1, ACT_BLOCKS:BLOCKS, :], in0=zT[:, b0 + ACT_BLOCKS : b0 + BLOCKS, :],
+                scalar1=neg_mu[:, 2 * q + 1 : 2 * q + 2],
+            )
+
+        def centre_scalar(k):
+            q, gg = divmod(k, GROUPS)
+            zcT = centred[k]
+            b0 = gg * BLOCKS
             nc.scalar.activation(
-                out=zcT[:], in_=zT[:, b0 : b0 + BLOCKS, :], func=ACTF.Identity,
+                out=zcT[:, 0, :, :], in_=zT[:, b0 : b0 + BLOCKS, :], func=ACTF.Identity,
                 bias=neg_mu[:, 2 * q : 2 * q + 1], scale=1.0,
+            )
+            nc.scalar.activation(
+                out=zcT[:, 1, 0:ACT_BLOCKS, :], in_=zT[:, b0 : b0 + ACT_BLOCKS, :], func=ACTF.Identity,
+                bias=neg_mu[:, 2 * q + 1 : 2 * q + 2], scale=1.0,
             )
 
         def fill(k, g4):
-            q, gg = divmod(k, GROUPS)
             zcT = centred[k]
             bank = ps_z.tile([P, 2, PACK, D], F32, name="bank")
-            for jj in range(2):
-                nc.tensor.transpose(
-                    bank[:, 0, 2 * jj : 2 * jj + 2, :].rearrange("p a d -> p (a d)"),
-                    zcT[:, 2 * g4 + jj, :],
-                    ident_f[:],
-                )
-            for jj in range(2):
-                region = bank[:, 1, 2 * jj : 2 * jj + 2, :].rearrange("p a d -> p (a d)")
-                nc.tensor.matmul(
-                    out=region, lhsT=neg_mu_wide[:, 2 * q + 1, :], rhs=ident_f[:],
-                    is_transpose=True, start=True, stop=False,
-                )
-                nc.tensor.matmul(
-                    out=region, lhsT=zT[:, gg * BLOCKS + 2 * g4 + jj, :], rhs=ident_f[:],
-                    is_transpose=True, start=False, stop=True,
-                )
+            for c2 in range(2):
+                for jj in range(2):
+                    nc.tensor.transpose(
+                        bank[:, c2, 2 * jj : 2 * jj + 2, :].rearrange("p a d -> p (a d)"),
+                        zcT[:, c2, 2 * g4 + jj, :],
+                        ident_f[:],
+                    )
             banks[(k, g4)] = bank
 
         def drain_zc(k, g4):
@@ -176,18 +174,28 @@ def tile_gmmestimationnetwork_pa_kernel(tc, z_batch, gamma, mu, gamma_mass, out)
             )
             quantised[k] = (codes, scales)
 
-        def multiply(k):
+        def multiply(k, half):
             q, gg = divmod(k, GROUPS)
             codes, scales = quantised[k]
-            for g4 in range(GROUP):
+            if gg == 0 and half == 0:
+                accs[q] = ps_acc.tile([P, MX_N], F32, name="acc")
+            for g4 in range(2 * half, 2 * half + 2):
                 g = gg * GROUP + g4
-                zc_cols = slice(g4 * P, (g4 + 1) * P)
+                zc_cols = slice(g4 * P, g4 * P + MX_N)
                 gz_cols = slice((GROUP + g4) * P, (GROUP + g4 + 1) * P)
                 nc.tensor.matmul_mx(
-                    out=acc[:, q, :],
+                    out=accs[q][:],
                     lhsT=codes[:, gz_cols].bitcast(FP8X4), lhsT_scale=scales[:, gz_cols],
                     rhs=codes[:, zc_cols].bitcast(FP8X4), rhs_scale=scales[:, zc_cols],
                     start=(g == 0), stop=(g == PASSES - 1),
+                )
+
+        def finish(q):
+            for c2 in range(2):
+                rows = slice(c2 * D, (c2 + 1) * D)
+                nc.vector.tensor_scalar_mul(
+                    out=res[rows, q, :], in0=accs[q][rows, c2 * D : (c2 + 1) * D],
+                    scalar1=inv_mass[rows, 2 * q + c2 : 2 * q + c2 + 1],
                 )
 
         TOTAL = PAIRS * GROUPS
@@ -209,18 +217,22 @@ def tile_gmmestimationnetwork_pa_kernel(tc, z_batch, gamma, mu, gamma_mass, out)
         def body():
             for gg in range(3):
                 zt_transposes(gg)
-                zt_evacuate_vector(gg)
-                zt_evacuate_scalar(gg)
+                zt_evacuate(gg)
             for k in range(2):
+                centre_vector(k)
                 centre_scalar(k)
             for u in range(GROUP):
                 fill_u(u)
-            for i in range(TOTAL + 1):
+            for i in range(TOTAL + 2):
                 u0 = GROUP * i
                 live = i < TOTAL
                 gz_u(u0 - 2)
                 fill_u(u0 + 4)
+                if 2 <= i:
+                    multiply(i - 2, 1)
                 gz_u(u0 - 1)
+                if 2 <= i and (i - 2) % GROUPS == GROUPS - 1:
+                    finish((i - 2) // GROUPS)
                 fill_u(u0 + 5)
                 if live:
                     zc_u(u0)
@@ -228,13 +240,13 @@ def tile_gmmestimationnetwork_pa_kernel(tc, z_batch, gamma, mu, gamma_mass, out)
                     fill_u(u0 + 6)
                 if i + 3 < GROUPS:
                     zt_transposes(i + 3)
-                if i >= 1:
+                if 1 <= i <= TOTAL:
                     quantise(i - 1)
-                    multiply(i - 1)
+                    multiply(i - 1, 0)
                 if live:
                     zc_u(u0 + 1)
-                    if i + 3 < GROUPS:
-                        zt_evacuate_vector(i + 3)
+                    if i + 2 < TOTAL:
+                        centre_vector(i + 2)
                     gz_u(u0 + 1)
                     fill_u(u0 + 7)
                     zc_u(u0 + 2)
@@ -242,7 +254,7 @@ def tile_gmmestimationnetwork_pa_kernel(tc, z_batch, gamma, mu, gamma_mass, out)
                     if i + 2 < TOTAL:
                         centre_scalar(i + 2)
                     if i + 3 < GROUPS:
-                        zt_evacuate_scalar(i + 3)
+                        zt_evacuate(i + 3)
 
         if PIN:
             with tc.manual_schedule():
@@ -250,13 +262,4 @@ def tile_gmmestimationnetwork_pa_kernel(tc, z_batch, gamma, mu, gamma_mass, out)
         else:
             body()
 
-        res = const.tile([P, PAIRS, D], F32)
-        for c2 in range(2):
-            rows = slice(c2 * D, (c2 + 1) * D)
-            nc.vector.tensor_tensor(
-                out=res[rows, :, :],
-                in0=acc[rows, :, c2 * D : (c2 + 1) * D],
-                in1=inv_mass[rows, :].rearrange("p (q c) -> p q c", c=2)[:, :, c2 : c2 + 1].to_broadcast([D, PAIRS, D]),
-                op=ALU.mult,
-            )
         nc.sync.dma_start(out=out.rearrange("(q c) i j -> (c i) q j", c=2), in_=res[:])

@@ -24,7 +24,7 @@ WIDTH = 2 * D * PACK
 CHUNK = 16
 ZBUFS = 4
 BANKS = 6
-ACT_BLOCKS = 3
+EVAC_ACT = 4
 PIN = True
 MX_N = 512
 
@@ -37,6 +37,7 @@ def tile_gmmestimationnetwork_pa_kernel(tc, z_batch, gamma, mu, gamma_mass, out)
         const = ctx.enter_context(tc.tile_pool(name="const", bufs=1))
         stage = ctx.enter_context(tc.tile_pool(name="stage", bufs=ZBUFS))
         work = ctx.enter_context(tc.tile_pool(name="work", bufs=3))
+        late = ctx.enter_context(tc.tile_pool(name="late", bufs=4))
         ps_t = ctx.enter_context(tc.psum_pool(name="ps_t", bufs=1))
         ps_z = ctx.enter_context(tc.psum_pool(name="ps_z", bufs=BANKS))
         ps_acc = ctx.enter_context(tc.psum_pool(name="ps_acc", bufs=1))
@@ -92,6 +93,7 @@ def tile_gmmestimationnetwork_pa_kernel(tc, z_batch, gamma, mu, gamma_mass, out)
         zT = const.tile([P, PASSES * 2, P], BF16)
         res = const.tile([P, PAIRS, D], F32)
         accs = {}
+        tick = const.tile([P, 1], F32)
 
         zt_banks = {}
         centred = {}
@@ -108,43 +110,47 @@ def tile_gmmestimationnetwork_pa_kernel(tc, z_batch, gamma, mu, gamma_mass, out)
                 nc.tensor.transpose(zt_ps[:, b, :], zs[:, gl, jj * P : (jj + 1) * P], ident_bf[:])
             zt_banks[gg] = zt_ps
 
-        def zt_evacuate(gg):
-            nc.scalar.copy(out=zT[:, gg * BLOCKS : (gg + 1) * BLOCKS, :], in_=zt_banks[gg][:])
+        def zt_evacuate_vector(gg):
+            b0 = gg * BLOCKS
+            nc.vector.tensor_copy(out=zT[:, b0 + EVAC_ACT : b0 + BLOCKS, :], in_=zt_banks[gg][:, EVAC_ACT:BLOCKS, :])
+
+        def zt_evacuate_scalar(gg):
+            b0 = gg * BLOCKS
+            nc.scalar.copy(out=zT[:, b0 : b0 + EVAC_ACT, :], in_=zt_banks[gg][:, 0:EVAC_ACT, :])
             nxt = (gg * GROUP) // CHUNK + ZBUFS
             if (gg * GROUP) % CHUNK == CHUNK - GROUP and nxt < PASSES // CHUNK:
                 load_z(nxt)
 
-        def centre_vector(k):
+        def centre_gpsimd(k):
             q, gg = divmod(k, GROUPS)
-            zcT = work.tile([P, 2, BLOCKS, P], F32, name="zcT")
-            centred[k] = zcT
+            zc1 = late.tile([P, BLOCKS, P], F32, name="zc1")
+            centred[(k, 1)] = zc1
             b0 = gg * BLOCKS
-            nc.vector.tensor_scalar_add(
-                out=zcT[:, 1, ACT_BLOCKS:BLOCKS, :], in0=zT[:, b0 + ACT_BLOCKS : b0 + BLOCKS, :],
-                scalar1=neg_mu[:, 2 * q + 1 : 2 * q + 2],
+            nc.gpsimd.tensor_scalar(
+                out=zc1[:], in0=zT[:, b0 : b0 + BLOCKS, :], scalar1=1.0,
+                scalar2=neg_mu[:, 2 * q + 1 : 2 * q + 2], op0=ALU.mult, op1=ALU.add,
             )
 
         def centre_scalar(k):
             q, gg = divmod(k, GROUPS)
-            zcT = centred[k]
+            zc0 = work.tile([P, BLOCKS, P], F32, name="zc0")
+            centred[(k, 0)] = zc0
             b0 = gg * BLOCKS
             nc.scalar.activation(
-                out=zcT[:, 0, :, :], in_=zT[:, b0 : b0 + BLOCKS, :], func=ACTF.Identity,
+                out=zc0[:], in_=zT[:, b0 : b0 + BLOCKS, :], func=ACTF.Identity,
                 bias=neg_mu[:, 2 * q : 2 * q + 1], scale=1.0,
             )
-            nc.scalar.activation(
-                out=zcT[:, 1, 0:ACT_BLOCKS, :], in_=zT[:, b0 : b0 + ACT_BLOCKS, :], func=ACTF.Identity,
-                bias=neg_mu[:, 2 * q + 1 : 2 * q + 2], scale=1.0,
-            )
+
+        def after_quantise(k):
+            nc.gpsimd.tensor_copy(out=tick[:], in_=quantised[k][0][:, 0:1].bitcast(F32))
 
         def fill(k, g4):
-            zcT = centred[k]
             bank = ps_z.tile([P, 2, PACK, D], F32, name="bank")
             for c2 in range(2):
                 for jj in range(2):
                     nc.tensor.transpose(
                         bank[:, c2, 2 * jj : 2 * jj + 2, :].rearrange("p a d -> p (a d)"),
-                        zcT[:, c2, 2 * g4 + jj, :],
+                        centred[(k, c2)][:, 2 * g4 + jj, :],
                         ident_f[:],
                     )
             banks[(k, g4)] = bank
@@ -215,12 +221,14 @@ def tile_gmmestimationnetwork_pa_kernel(tc, z_batch, gamma, mu, gamma_mass, out)
                 drain_gz(u // GROUP, u % GROUP)
 
         def body():
-            for gg in range(3):
+            for gg in range(4):
                 zt_transposes(gg)
-                zt_evacuate(gg)
+                zt_evacuate_vector(gg)
+                zt_evacuate_scalar(gg)
             for k in range(2):
-                centre_vector(k)
                 centre_scalar(k)
+            for k in range(3):
+                centre_gpsimd(k)
             for u in range(GROUP):
                 fill_u(u)
             for i in range(TOTAL + 2):
@@ -238,23 +246,27 @@ def tile_gmmestimationnetwork_pa_kernel(tc, z_batch, gamma, mu, gamma_mass, out)
                     zc_u(u0)
                     gz_u(u0)
                     fill_u(u0 + 6)
-                if i + 3 < GROUPS:
-                    zt_transposes(i + 3)
+                if i + 4 < GROUPS:
+                    zt_transposes(i + 4)
                 if 1 <= i <= TOTAL:
                     quantise(i - 1)
                     multiply(i - 1, 0)
+                    if i + 3 < TOTAL:
+                        after_quantise(i - 1)
+                if i + 3 < TOTAL:
+                    centre_gpsimd(i + 3)
                 if live:
                     zc_u(u0 + 1)
-                    if i + 2 < TOTAL:
-                        centre_vector(i + 2)
+                    if i + 4 < GROUPS:
+                        zt_evacuate_vector(i + 4)
                     gz_u(u0 + 1)
                     fill_u(u0 + 7)
                     zc_u(u0 + 2)
                     zc_u(u0 + 3)
                     if i + 2 < TOTAL:
                         centre_scalar(i + 2)
-                    if i + 3 < GROUPS:
-                        zt_evacuate(i + 3)
+                    if i + 4 < GROUPS:
+                        zt_evacuate_scalar(i + 4)
 
         if PIN:
             with tc.manual_schedule():

@@ -21,8 +21,8 @@ GROUPS = PASSES // GROUP
 PAIRS = K // 2
 BLOCKS = 2 * GROUP
 WIDTH = 2 * D * PACK
-CHUNK = 16
-ZBUFS = 4
+CHUNK = 4
+ZBUFS = 8
 BANKS = 6
 EVAC_ACT = 4
 PIN = True
@@ -56,6 +56,11 @@ def tile_gmmestimationnetwork_pa_kernel(tc, z_batch, gamma, mu, gamma_mass, out)
         make_identity(nc, ident_bf[:])
         ident_f = const.tile([P, P], F32)
         make_identity(nc, ident_f[:])
+
+        perm_f = const.tile([P, P], F32)
+        nc.vector.tensor_copy(
+            out=perm_f[:].rearrange("k (d a) -> k d a", a=2), in_=ident_f[:].rearrange("k (a d) -> k d a", a=2)
+        )
 
         mu_rows = const.tile([P, P], BF16)
         nc.vector.memset(mu_rows[:], 0.0)
@@ -93,7 +98,7 @@ def tile_gmmestimationnetwork_pa_kernel(tc, z_batch, gamma, mu, gamma_mass, out)
         zT = const.tile([P, PASSES * 2, P], BF16)
         res = const.tile([P, PAIRS, D], F32)
         accs = {}
-        tick = const.tile([P, 1], F32)
+        tick = const.tile([P, 1], BF16)
 
         zt_banks = {}
         centred = {}
@@ -141,24 +146,24 @@ def tile_gmmestimationnetwork_pa_kernel(tc, z_batch, gamma, mu, gamma_mass, out)
                 bias=neg_mu[:, 2 * q : 2 * q + 1], scale=1.0,
             )
 
-        def after_quantise(k):
-            nc.gpsimd.tensor_copy(out=tick[:], in_=quantised[k][0][:, 0:1].bitcast(F32))
+        def follow_vector(k):
+            nc.gpsimd.tensor_copy(out=tick[:], in_=qins[k][:, 1, 0, 0:1])
 
         def fill(k, g4):
-            bank = ps_z.tile([P, 2, PACK, D], F32, name="bank")
+            bank = ps_z.tile([P, 2, D, PACK], F32, name="bank")
             for c2 in range(2):
                 for jj in range(2):
                     nc.tensor.transpose(
-                        bank[:, c2, 2 * jj : 2 * jj + 2, :].rearrange("p a d -> p (a d)"),
+                        bank[:, c2, :, 2 * jj : 2 * jj + 2],
                         centred[(k, c2)][:, 2 * g4 + jj, :],
-                        ident_f[:],
+                        perm_f[:],
                     )
             banks[(k, g4)] = bank
 
         def drain_zc(k, g4):
             nc.scalar.copy(
-                out=qins[k][:, 0, g4, :].rearrange("p (c d j) -> p c d j", c=2, j=PACK),
-                in_=banks[(k, g4)][:].rearrange("p c j d -> p c d j"),
+                out=qins[k][:, 0, g4, :],
+                in_=banks[(k, g4)][:].rearrange("p c d j -> p (c d j)"),
             )
 
         def drain_gz(k, g4):
@@ -166,7 +171,7 @@ def tile_gmmestimationnetwork_pa_kernel(tc, z_batch, gamma, mu, gamma_mass, out)
             g = gg * GROUP + g4
             nc.vector.tensor_tensor(
                 out=qins[k][:, 1, g4, :].rearrange("p (c d j) -> p c d j", c=2, j=PACK),
-                in0=banks[(k, g4)][:].rearrange("p c j d -> p c d j"),
+                in0=banks[(k, g4)][:],
                 in1=gam[:, g, 2 * q : 2 * q + 2, :].unsqueeze(2).to_broadcast([P, 2, D, PACK]),
                 op=ALU.mult,
             )
@@ -225,10 +230,10 @@ def tile_gmmestimationnetwork_pa_kernel(tc, z_batch, gamma, mu, gamma_mass, out)
                 zt_transposes(gg)
                 zt_evacuate_vector(gg)
                 zt_evacuate_scalar(gg)
-            for k in range(2):
-                centre_scalar(k)
-            for k in range(3):
-                centre_gpsimd(k)
+                if gg < 2:
+                    centre_scalar(gg)
+                if gg < 3:
+                    centre_gpsimd(gg)
             for u in range(GROUP):
                 fill_u(u)
             for i in range(TOTAL + 2):
@@ -251,9 +256,8 @@ def tile_gmmestimationnetwork_pa_kernel(tc, z_batch, gamma, mu, gamma_mass, out)
                 if 1 <= i <= TOTAL:
                     quantise(i - 1)
                     multiply(i - 1, 0)
-                    if i + 3 < TOTAL:
-                        after_quantise(i - 1)
                 if i + 3 < TOTAL:
+                    follow_vector(i)
                     centre_gpsimd(i + 3)
                 if live:
                     zc_u(u0 + 1)

@@ -24,7 +24,7 @@ WIDTH = 2 * D * PACK
 CHUNK = 4
 ZBUFS = 8
 BANKS = 6
-EVAC_ACT = 4
+EVAC_ACT = 6
 PIN = True
 MX_N = 512
 
@@ -217,7 +217,7 @@ def tile_gmmestimationnetwork_pa_kernel(tc, z_batch, gamma, mu, gamma_mass, out)
                 fill(u // GROUP, u % GROUP)
 
         def zc_u(u):
-            if u % GROUP == 0:
+            if u // GROUP not in qins:
                 qins[u // GROUP] = work.tile([P, 2, GROUP, WIDTH], BF16, name="qin", align_bytes=64)
             drain_zc(u // GROUP, u % GROUP)
 
@@ -248,6 +248,7 @@ def tile_gmmestimationnetwork_pa_kernel(tc, z_batch, gamma, mu, gamma_mass, out)
                     finish((i - 2) // GROUPS)
                 fill_u(u0 + 5)
                 if live:
+                    zc_u(u0 + 1)
                     zc_u(u0)
                     gz_u(u0)
                     fill_u(u0 + 6)
@@ -260,13 +261,12 @@ def tile_gmmestimationnetwork_pa_kernel(tc, z_batch, gamma, mu, gamma_mass, out)
                     follow_vector(i)
                     centre_gpsimd(i + 3)
                 if live:
-                    zc_u(u0 + 1)
                     if i + 4 < GROUPS:
                         zt_evacuate_vector(i + 4)
                     gz_u(u0 + 1)
                     fill_u(u0 + 7)
-                    zc_u(u0 + 2)
                     zc_u(u0 + 3)
+                    zc_u(u0 + 2)
                     if i + 2 < TOTAL:
                         centre_scalar(i + 2)
                     if i + 4 < GROUPS:

@@ -11,44 +11,46 @@ FP8X4 = mybir.dt.float8_e4m3fn_x4
 ALU = mybir.AluOpType
 ACTF = mybir.ActivationFunctionType
 
-N, D, K = 65536, 64, 8
+SAMPLES, DIM, COMPONENTS = 65536, 64, 8
 P = 128
 PACK = 4
 K_PASS = P * PACK
-PASSES = N // K_PASS
+PASSES = SAMPLES // K_PASS
 GROUP = 4
 GROUPS = PASSES // GROUP
-PAIRS = K // 2
+PAIRS = COMPONENTS // 2
+STEPS = PAIRS * GROUPS
+UNITS = STEPS * GROUP
 BLOCKS = 2 * GROUP
-WIDTH = 2 * D * PACK
-CHUNK = 4
-ZBUFS = 8
+WIDTH = 2 * DIM * PACK
+Z_AHEAD = 8
 BANKS = 6
-EVAC_ACT = 6
-PIN = True
-MX_N = 512
+SCALAR_BLOCKS = 5
+LEAD = 4
+GAMMA_PARTS = 4
+MX_COLUMNS = 512
 
-FLOPS = 2 * K * N * D * D
+FLOPS = 2 * COMPONENTS * SAMPLES * DIM * DIM
 
 
 def tile_gmmestimationnetwork_pa_kernel(tc, z_batch, gamma, mu, gamma_mass, out):
     nc = tc.nc
     with ExitStack() as ctx:
         const = ctx.enter_context(tc.tile_pool(name="const", bufs=1))
-        stage = ctx.enter_context(tc.tile_pool(name="stage", bufs=ZBUFS))
+        stage = ctx.enter_context(tc.tile_pool(name="stage", bufs=Z_AHEAD))
         work = ctx.enter_context(tc.tile_pool(name="work", bufs=3))
         late = ctx.enter_context(tc.tile_pool(name="late", bufs=4))
         ps_t = ctx.enter_context(tc.psum_pool(name="ps_t", bufs=1))
         ps_z = ctx.enter_context(tc.psum_pool(name="ps_z", bufs=BANKS))
         ps_acc = ctx.enter_context(tc.psum_pool(name="ps_acc", bufs=1))
 
-        chunks = {}
+        z_groups = {}
 
-        def load_z(ch):
-            zs = stage.tile([P, CHUNK, PACK * D], BF16, name="zs")
-            rows = z_batch[ch * CHUNK * K_PASS : (ch + 1) * CHUNK * K_PASS, :]
-            nc.sync.dma_start(out=zs[:], in_=rows.rearrange("(g p j) d -> p g (j d)", p=P, j=PACK))
-            chunks[ch] = zs
+        def load_z(gg):
+            zs = stage.tile([P, GROUP, PACK * DIM], BF16, name="zs")
+            z_rows = z_batch[gg * GROUP * K_PASS : (gg + 1) * GROUP * K_PASS, :]
+            nc.sync.dma_start(out=zs[:], in_=z_rows.rearrange("(g p j) d -> p g (j d)", p=P, j=PACK))
+            z_groups[gg] = zs
 
         load_z(0)
 
@@ -64,40 +66,39 @@ def tile_gmmestimationnetwork_pa_kernel(tc, z_batch, gamma, mu, gamma_mass, out)
 
         mu_rows = const.tile([P, P], BF16)
         nc.vector.memset(mu_rows[:], 0.0)
-        nc.scalar.dma_start(out=mu_rows[0:K, 0:D], in_=mu)
-        nc.scalar.dma_start(out=mu_rows[0:K, D : 2 * D], in_=mu)
-        mass_bf = const.tile([P, K], BF16)
+        nc.scalar.dma_start(out=mu_rows[0:COMPONENTS, 0:DIM], in_=mu)
+        nc.scalar.dma_start(out=mu_rows[0:COMPONENTS, DIM : 2 * DIM], in_=mu)
+        mass_bf = const.tile([P, COMPONENTS], BF16)
         nc.scalar.dma_start(out=mass_bf[:], in_=gamma_mass.partition_broadcast(P))
 
-        gam_nat = const.tile([P, PASSES, PACK, K], BF16)
-        gam = const.tile([P, PASSES, K, PACK], BF16)
-        QG = PASSES // 4
-        for s in range(4):
-            rows = gamma[s * QG * K_PASS : (s + 1) * QG * K_PASS, :]
+        gam_nat = const.tile([P, PASSES, PACK, COMPONENTS], BF16)
+        gam = const.tile([P, PASSES, COMPONENTS, PACK], BF16)
+        part = PASSES // GAMMA_PARTS
+        for s in range(GAMMA_PARTS):
+            gamma_rows = gamma[s * part * K_PASS : (s + 1) * part * K_PASS, :]
             nc.scalar.dma_start(
-                out=gam_nat[:, s * QG : (s + 1) * QG, :, :].rearrange("p g j c -> p g (j c)"),
-                in_=rows.rearrange("(g p j) c -> p g (j c)", p=P, j=PACK),
+                out=gam_nat[:, s * part : (s + 1) * part, :, :].rearrange("p g j c -> p g (j c)"),
+                in_=gamma_rows.rearrange("(g p j) c -> p g (j c)", p=P, j=PACK),
             )
-        for ch in range(1, ZBUFS):
-            load_z(ch)
+        for gg in range(1, Z_AHEAD):
+            load_z(gg)
 
         mu_ps = ps_t.tile([P, P], BF16, tag="zt")
         nc.tensor.transpose(mu_ps[:], mu_rows[:], ident_bf[:])
-        neg_mu = const.tile([P, K], F32)
-        nc.vector.tensor_scalar_mul(out=neg_mu[:], in0=mu_ps[:, 0:K], scalar1=-1.0)
-        mass_f = const.tile([P, K], F32)
-        nc.vector.tensor_copy(out=mass_f[:], in_=mass_bf[:])
-        inv_mass = const.tile([P, K], F32)
+        neg_mu = const.tile([P, COMPONENTS], F32)
+        nc.vector.tensor_scalar_mul(out=neg_mu[:], in0=mu_ps[:, 0:COMPONENTS], scalar1=-1.0)
+        mass_f = const.tile([P, COMPONENTS], F32)
+        nc.scalar.copy(out=mass_f[:], in_=mass_bf[:])
+        inv_mass = const.tile([P, COMPONENTS], F32)
         nc.vector.reciprocal(out=inv_mass[:], in_=mass_f[:])
-        for s in range(4):
+        for s in range(GAMMA_PARTS):
             nc.vector.tensor_copy(
-                out=gam[:, s * QG : (s + 1) * QG, :, :],
-                in_=gam_nat[:, s * QG : (s + 1) * QG, :, :].rearrange("p g j c -> p g c j"),
+                out=gam[:, s * part : (s + 1) * part, :, :],
+                in_=gam_nat[:, s * part : (s + 1) * part, :, :].rearrange("p g j c -> p g c j"),
             )
 
         zT = const.tile([P, PASSES * 2, P], BF16)
-        res = const.tile([P, PAIRS, D], F32)
-        accs = {}
+        res = const.tile([P, PAIRS, DIM], F32)
         tick = const.tile([P, 1], BF16)
 
         zt_banks = {}
@@ -105,94 +106,123 @@ def tile_gmmestimationnetwork_pa_kernel(tc, z_batch, gamma, mu, gamma_mass, out)
         banks = {}
         qins = {}
         quantised = {}
+        accs = {}
 
-        def zt_transposes(gg):
-            zs = chunks[(gg * GROUP) // CHUNK]
+        def transpose_z(gg):
+            if not 0 <= gg < GROUPS:
+                return
+            zs = z_groups[gg]
             zt_ps = ps_t.tile([P, BLOCKS, P], BF16, tag="zt")
             for b in range(BLOCKS):
-                gl = (gg * GROUP + b // 2) % CHUNK
-                jj = b % 2
-                nc.tensor.transpose(zt_ps[:, b, :], zs[:, gl, jj * P : (jj + 1) * P], ident_bf[:])
+                g4, jj = divmod(b, 2)
+                nc.tensor.transpose(zt_ps[:, b, :], zs[:, g4, jj * P : (jj + 1) * P], ident_bf[:])
             zt_banks[gg] = zt_ps
 
-        def zt_evacuate_vector(gg):
-            b0 = gg * BLOCKS
-            nc.vector.tensor_copy(out=zT[:, b0 + EVAC_ACT : b0 + BLOCKS, :], in_=zt_banks[gg][:, EVAC_ACT:BLOCKS, :])
+        def evacuate_z(gg):
+            if not 0 <= gg < GROUPS:
+                return
+            nc.scalar.copy(out=zT[:, gg * BLOCKS : (gg + 1) * BLOCKS, :], in_=zt_banks[gg][:])
+            if gg + Z_AHEAD < GROUPS:
+                load_z(gg + Z_AHEAD)
 
-        def zt_evacuate_scalar(gg):
-            b0 = gg * BLOCKS
-            nc.scalar.copy(out=zT[:, b0 : b0 + EVAC_ACT, :], in_=zt_banks[gg][:, 0:EVAC_ACT, :])
-            nxt = (gg * GROUP) // CHUNK + ZBUFS
-            if (gg * GROUP) % CHUNK == CHUNK - GROUP and nxt < PASSES // CHUNK:
-                load_z(nxt)
-
-        def centre_gpsimd(k):
-            q, gg = divmod(k, GROUPS)
-            zc1 = late.tile([P, BLOCKS, P], F32, name="zc1")
-            centred[(k, 1)] = zc1
+        def centre_gpsimd(zc, step, c2, first_block):
+            q, gg = divmod(step, GROUPS)
             b0 = gg * BLOCKS
             nc.gpsimd.tensor_scalar(
-                out=zc1[:], in0=zT[:, b0 : b0 + BLOCKS, :], scalar1=1.0,
-                scalar2=neg_mu[:, 2 * q + 1 : 2 * q + 2], op0=ALU.mult, op1=ALU.add,
+                out=zc[:, first_block:BLOCKS, :], in0=zT[:, b0 + first_block : b0 + BLOCKS, :], scalar1=1.0,
+                scalar2=neg_mu[:, 2 * q + c2 : 2 * q + c2 + 1], op0=ALU.mult, op1=ALU.add,
             )
 
-        def centre_scalar(k):
-            q, gg = divmod(k, GROUPS)
+        def centre_second(step):
+            if not 0 <= step < STEPS:
+                return
+            zc1 = late.tile([P, BLOCKS, P], F32, name="zc1")
+            centred[(step, 1)] = zc1
+            centre_gpsimd(zc1, step, 1, 0)
+
+        def scalar_blocks(step):
+            return SCALAR_BLOCKS if step < GROUPS else BLOCKS
+
+        def centre_first_gpsimd(step):
+            if not 0 <= step < STEPS:
+                return
             zc0 = work.tile([P, BLOCKS, P], F32, name="zc0")
-            centred[(k, 0)] = zc0
+            centred[(step, 0)] = zc0
+            if scalar_blocks(step) < BLOCKS:
+                centre_gpsimd(zc0, step, 0, scalar_blocks(step))
+
+        def centre_first_scalar(step):
+            if not 0 <= step < STEPS:
+                return
+            q, gg = divmod(step, GROUPS)
             b0 = gg * BLOCKS
+            blocks = scalar_blocks(step)
             nc.scalar.activation(
-                out=zc0[:], in_=zT[:, b0 : b0 + BLOCKS, :], func=ACTF.Identity,
-                bias=neg_mu[:, 2 * q : 2 * q + 1], scale=1.0,
+                out=centred[(step, 0)][:, 0:blocks, :], in_=zT[:, b0 : b0 + blocks, :],
+                func=ACTF.Identity, bias=neg_mu[:, 2 * q : 2 * q + 1], scale=1.0,
             )
 
-        def follow_vector(k):
-            nc.gpsimd.tensor_copy(out=tick[:], in_=qins[k][:, 1, 0, 0:1])
+        def follow_vector(step):
+            if not 0 <= step < STEPS - 3:
+                return
+            nc.gpsimd.tensor_copy(out=tick[:], in_=qins[step][:, 1, 0, 0:1])
 
-        def fill(k, g4):
-            bank = ps_z.tile([P, 2, D, PACK], F32, name="bank")
+        def fill(u):
+            if not 0 <= u < UNITS:
+                return
+            step, g4 = divmod(u, GROUP)
+            bank = ps_z.tile([P, 2, DIM, PACK], F32, name="bank")
             for c2 in range(2):
                 for jj in range(2):
                     nc.tensor.transpose(
                         bank[:, c2, :, 2 * jj : 2 * jj + 2],
-                        centred[(k, c2)][:, 2 * g4 + jj, :],
+                        centred[(step, c2)][:, 2 * g4 + jj, :],
                         perm_f[:],
                     )
-            banks[(k, g4)] = bank
+            banks[u] = bank
 
-        def drain_zc(k, g4):
-            nc.scalar.copy(
-                out=qins[k][:, 0, g4, :],
-                in_=banks[(k, g4)][:].rearrange("p c d j -> p (c d j)"),
-            )
+        def copy_zc(u):
+            if not 0 <= u < UNITS:
+                return
+            step, g4 = divmod(u, GROUP)
+            if g4 == 0:
+                qins[step] = work.tile([P, 2, GROUP, WIDTH], BF16, name="qin", align_bytes=64)
+            nc.scalar.copy(out=qins[step][:, 0, g4, :], in_=banks[u][:].rearrange("p c d j -> p (c d j)"))
 
-        def drain_gz(k, g4):
-            q, gg = divmod(k, GROUPS)
+        def multiply_gamma(u):
+            if not 0 <= u < UNITS:
+                return
+            step, g4 = divmod(u, GROUP)
+            q, gg = divmod(step, GROUPS)
             g = gg * GROUP + g4
             nc.vector.tensor_tensor(
-                out=qins[k][:, 1, g4, :].rearrange("p (c d j) -> p c d j", c=2, j=PACK),
-                in0=banks[(k, g4)][:],
-                in1=gam[:, g, 2 * q : 2 * q + 2, :].unsqueeze(2).to_broadcast([P, 2, D, PACK]),
+                out=qins[step][:, 1, g4, :].rearrange("p (c d j) -> p c d j", c=2, j=PACK),
+                in0=banks[u][:],
+                in1=gam[:, g, 2 * q : 2 * q + 2, :].unsqueeze(2).to_broadcast([P, 2, DIM, PACK]),
                 op=ALU.mult,
             )
 
-        def quantise(k):
+        def quantise(step):
+            if not 0 <= step < STEPS:
+                return
             codes = work.tile([P, 2 * GROUP * P], U32, name="codes", align_bytes=64)
             scales = work.tile([P, 2 * GROUP * P], U8, name="scales", align_bytes=64)
             nc.vector.quantize_mx(
                 out=codes[:].bitcast(FP8X4), scales=scales[:],
-                in_=qins[k][:].rearrange("p a g w -> p (a g w)"),
+                in_=qins[step][:].rearrange("p a g w -> p (a g w)"),
             )
-            quantised[k] = (codes, scales)
+            quantised[step] = (codes, scales)
 
-        def multiply(k, half):
-            q, gg = divmod(k, GROUPS)
-            codes, scales = quantised[k]
+        def multiply(step, half):
+            if not 0 <= step < STEPS:
+                return
+            q, gg = divmod(step, GROUPS)
+            codes, scales = quantised[step]
             if gg == 0 and half == 0:
-                accs[q] = ps_acc.tile([P, MX_N], F32, name="acc")
+                accs[q] = ps_acc.tile([P, MX_COLUMNS], F32, name="acc")
             for g4 in range(2 * half, 2 * half + 2):
                 g = gg * GROUP + g4
-                zc_cols = slice(g4 * P, g4 * P + MX_N)
+                zc_cols = slice(g4 * P, g4 * P + MX_COLUMNS)
                 gz_cols = slice((GROUP + g4) * P, (GROUP + g4 + 1) * P)
                 nc.tensor.matmul_mx(
                     out=accs[q][:],
@@ -201,81 +231,41 @@ def tile_gmmestimationnetwork_pa_kernel(tc, z_batch, gamma, mu, gamma_mass, out)
                     start=(g == 0), stop=(g == PASSES - 1),
                 )
 
-        def finish(q):
+        def finish(step):
+            q, gg = divmod(step, GROUPS)
+            if not (0 <= step and gg == GROUPS - 1):
+                return
             for c2 in range(2):
-                rows = slice(c2 * D, (c2 + 1) * D)
+                own = slice(c2 * DIM, (c2 + 1) * DIM)
                 nc.vector.tensor_scalar_mul(
-                    out=res[rows, q, :], in0=accs[q][rows, c2 * D : (c2 + 1) * D],
-                    scalar1=inv_mass[rows, 2 * q + c2 : 2 * q + c2 + 1],
+                    out=res[own, q, :], in0=accs[q][own, own],
+                    scalar1=inv_mass[own, 2 * q + c2 : 2 * q + c2 + 1],
                 )
 
-        TOTAL = PAIRS * GROUPS
-        UNITS = TOTAL * GROUP
-
-        def fill_u(u):
-            if 0 <= u < UNITS:
-                fill(u // GROUP, u % GROUP)
-
-        def zc_u(u):
-            if u // GROUP not in qins:
-                qins[u // GROUP] = work.tile([P, 2, GROUP, WIDTH], BF16, name="qin", align_bytes=64)
-            drain_zc(u // GROUP, u % GROUP)
-
-        def gz_u(u):
-            if 0 <= u < UNITS:
-                drain_gz(u // GROUP, u % GROUP)
-
-        def body():
-            for gg in range(4):
-                zt_transposes(gg)
-                zt_evacuate_vector(gg)
-                zt_evacuate_scalar(gg)
-                if gg < 2:
-                    centre_scalar(gg)
-                if gg < 3:
-                    centre_gpsimd(gg)
-            for u in range(GROUP):
-                fill_u(u)
-            for i in range(TOTAL + 2):
+        with tc.manual_schedule():
+            for i in range(-LEAD, STEPS + 2):
                 u0 = GROUP * i
-                live = i < TOTAL
-                gz_u(u0 - 2)
-                fill_u(u0 + 4)
-                if 2 <= i:
-                    multiply(i - 2, 1)
-                gz_u(u0 - 1)
-                if 2 <= i and (i - 2) % GROUPS == GROUPS - 1:
-                    finish((i - 2) // GROUPS)
-                fill_u(u0 + 5)
-                if live:
-                    zc_u(u0 + 1)
-                    zc_u(u0)
-                    gz_u(u0)
-                    fill_u(u0 + 6)
-                if i + 4 < GROUPS:
-                    zt_transposes(i + 4)
-                if 1 <= i <= TOTAL:
-                    quantise(i - 1)
-                    multiply(i - 1, 0)
-                if i + 3 < TOTAL:
-                    follow_vector(i)
-                    centre_gpsimd(i + 3)
-                if live:
-                    if i + 4 < GROUPS:
-                        zt_evacuate_vector(i + 4)
-                    gz_u(u0 + 1)
-                    fill_u(u0 + 7)
-                    zc_u(u0 + 3)
-                    zc_u(u0 + 2)
-                    if i + 2 < TOTAL:
-                        centre_scalar(i + 2)
-                    if i + 4 < GROUPS:
-                        zt_evacuate_scalar(i + 4)
-
-        if PIN:
-            with tc.manual_schedule():
-                body()
-        else:
-            body()
+                multiply_gamma(u0 - 2)
+                fill(u0 + 4)
+                multiply(i - 2, 1)
+                multiply_gamma(u0 - 1)
+                finish(i - 2)
+                fill(u0 + 5)
+                copy_zc(u0)
+                multiply_gamma(u0)
+                fill(u0 + 6)
+                transpose_z(i + LEAD)
+                quantise(i - 1)
+                multiply(i - 1, 0)
+                follow_vector(i)
+                centre_second(i + 3)
+                centre_first_gpsimd(i + 2)
+                copy_zc(u0 + 1)
+                multiply_gamma(u0 + 1)
+                fill(u0 + 7)
+                copy_zc(u0 + 2)
+                copy_zc(u0 + 3)
+                centre_first_scalar(i + 2)
+                evacuate_z(i + LEAD)
 
         nc.sync.dma_start(out=out.rearrange("(q c) i j -> (c i) q j", c=2), in_=res[:])

@@ -28,6 +28,7 @@ BANKS = 6
 SCALAR_BLOCKS = 5
 LEAD = 4
 GAMMA_PARTS = 4
+GAMMA_LEAD = 4
 MX_COLUMNS = 512
 
 FLOPS = 2 * COMPONENTS * SAMPLES * DIM * DIM
@@ -52,54 +53,65 @@ def tile_gmmestimationnetwork_pa_kernel(tc, z_batch, gamma, mu, gamma_mass, out)
             nc.sync.dma_start(out=zs[:], in_=z_rows.rearrange("(g p j) d -> p g (j d)", p=P, j=PACK))
             z_groups[gg] = zs
 
-        load_z(0)
-
-        ident_bf = const.tile([P, P], BF16)
-        make_identity(nc, ident_bf[:])
-        ident_f = const.tile([P, P], F32)
-        make_identity(nc, ident_f[:])
-
-        perm_f = const.tile([P, P], F32)
-        nc.vector.tensor_copy(
-            out=perm_f[:].rearrange("k (d a) -> k d a", a=2), in_=ident_f[:].rearrange("k (a d) -> k d a", a=2)
-        )
-
-        mu_rows = const.tile([P, P], BF16)
-        nc.vector.memset(mu_rows[:], 0.0)
-        nc.scalar.dma_start(out=mu_rows[0:COMPONENTS, 0:DIM], in_=mu)
-        nc.scalar.dma_start(out=mu_rows[0:COMPONENTS, DIM : 2 * DIM], in_=mu)
-        mass_bf = const.tile([P, COMPONENTS], BF16)
-        nc.scalar.dma_start(out=mass_bf[:], in_=gamma_mass.partition_broadcast(P))
-
         gam_nat = const.tile([P, PASSES, PACK, COMPONENTS], BF16)
         gam = const.tile([P, PASSES, COMPONENTS, PACK], BF16)
         part = PASSES // GAMMA_PARTS
-        for s in range(GAMMA_PARTS):
+
+        def load_gamma(s):
             gamma_rows = gamma[s * part * K_PASS : (s + 1) * part * K_PASS, :]
-            nc.scalar.dma_start(
+            nc.sync.dma_start(
                 out=gam_nat[:, s * part : (s + 1) * part, :, :].rearrange("p g j c -> p g (j c)"),
                 in_=gamma_rows.rearrange("(g p j) c -> p g (j c)", p=P, j=PACK),
             )
-        for gg in range(1, Z_AHEAD):
-            load_z(gg)
 
-        mu_ps = ps_t.tile([P, P], BF16, tag="zt")
-        nc.tensor.transpose(mu_ps[:], mu_rows[:], ident_bf[:])
-        neg_mu = const.tile([P, COMPONENTS], F32)
-        nc.vector.tensor_scalar_mul(out=neg_mu[:], in0=mu_ps[:, 0:COMPONENTS], scalar1=-1.0)
-        mass_f = const.tile([P, COMPONENTS], F32)
-        nc.scalar.copy(out=mass_f[:], in_=mass_bf[:])
-        inv_mass = const.tile([P, COMPONENTS], F32)
-        nc.vector.reciprocal(out=inv_mass[:], in_=mass_f[:])
-        for s in range(GAMMA_PARTS):
-            nc.vector.tensor_copy(
-                out=gam[:, s * part : (s + 1) * part, :, :],
-                in_=gam_nat[:, s * part : (s + 1) * part, :, :].rearrange("p g j c -> p g c j"),
-            )
+        def gamma_views(s):
+            passes = slice(s * part, (s + 1) * part)
+            return gam[:, passes, :, :], gam_nat[:, passes, :, :].rearrange("p g j c -> p g c j")
 
         zT = const.tile([P, PASSES * 2, P], BF16)
         res = const.tile([P, PAIRS, DIM], F32)
         tick = const.tile([P, 1], BF16)
+        ident_bf = const.tile([P, P], BF16)
+        ident_f = const.tile([P, P], F32)
+        perm_f = const.tile([P, P], F32)
+        mu_rows = const.tile([P, P], BF16)
+        mass_bf = const.tile([P, COMPONENTS], BF16)
+        neg_mu = const.tile([P, COMPONENTS], F32)
+        inv_mass = const.tile([P, COMPONENTS], F32)
+
+        def prologue():
+            load_z(0)
+            nc.vector.memset(mu_rows[:], 0.0)
+            nc.scalar.dma_start(out=mu_rows[0:COMPONENTS, 0:DIM], in_=mu)
+            nc.scalar.dma_start(out=mu_rows[0:COMPONENTS, DIM : 2 * DIM], in_=mu)
+            nc.vector.memset(tick[:], 0.0)
+            nc.scalar.activation(out=inv_mass[:, 0:1], in_=tick[:], func=ACTF.Identity, bias=0.0, scale=1.0)
+            make_identity(nc, ident_bf[:])
+            make_identity(nc, ident_f[:])
+            load_gamma(0)
+            for gg in range(1, Z_AHEAD):
+                load_z(gg)
+            for s in range(1, GAMMA_PARTS):
+                load_gamma(s)
+            nc.sync.dma_start(out=mass_bf[:], in_=gamma_mass.partition_broadcast(P))
+
+            mu_ps = ps_t.tile([P, P], BF16, tag="zt", name="mu_ps")
+            nc.tensor.transpose(mu_ps[:], mu_rows[:], ident_bf[:])
+            nc.vector.tensor_scalar_mul(out=neg_mu[:], in0=mu_ps[:, 0:COMPONENTS], scalar1=-1.0)
+            nc.vector.tensor_copy(
+                out=perm_f[:].rearrange("k (d a) -> k d a", a=2), in_=ident_f[:].rearrange("k (a d) -> k d a", a=2)
+            )
+            gam_part, nat_part = gamma_views(0)
+            nc.vector.tensor_copy(out=gam_part, in_=nat_part)
+
+        def regroup_gamma(step):
+            s, ahead = divmod(step + GAMMA_LEAD, part // GROUP)
+            if not (1 <= s < GAMMA_PARTS and ahead == 0):
+                return
+            gam_part, nat_part = gamma_views(s)
+            nc.gpsimd.tensor_scalar(
+                out=gam_part, in0=nat_part, scalar1=1.0, scalar2=0.0, op0=ALU.mult, op1=ALU.add
+            )
 
         zt_banks = {}
         centred = {}
@@ -243,12 +255,15 @@ def tile_gmmestimationnetwork_pa_kernel(tc, z_batch, gamma, mu, gamma_mass, out)
                 )
 
         with tc.manual_schedule():
+            prologue()
             for i in range(-LEAD, STEPS + 2):
                 u0 = GROUP * i
                 multiply_gamma(u0 - 2)
                 fill(u0 + 4)
                 multiply(i - 2, 1)
                 multiply_gamma(u0 - 1)
+                if i == GAMMA_LEAD:
+                    nc.vector.reciprocal(out=inv_mass[:], in_=mass_bf[:])
                 finish(i - 2)
                 fill(u0 + 5)
                 copy_zc(u0)
@@ -260,6 +275,7 @@ def tile_gmmestimationnetwork_pa_kernel(tc, z_batch, gamma, mu, gamma_mass, out)
                 follow_vector(i)
                 centre_second(i + 3)
                 centre_first_gpsimd(i + 2)
+                regroup_gamma(i)
                 copy_zc(u0 + 1)
                 multiply_gamma(u0 + 1)
                 fill(u0 + 7)

@@ -28,6 +28,7 @@ BANKS = 6
 SCALAR_BLOCKS = 5
 LEAD = 4
 GAMMA_PARTS = 4
+WARM_AHEAD = 3
 GAMMA_LEAD = 4
 MX_COLUMNS = 512
 
@@ -75,13 +76,20 @@ def tile_gmmestimationnetwork_pa_kernel(tc, z_batch, gamma, mu, gamma_mass, out)
         ident_f = const.tile([P, P], F32)
         perm_f = const.tile([P, P], F32)
         mu_rows = const.tile([P, P], BF16)
+        zeros = const.tile([P, MX_COLUMNS], BF16)
         mass_bf = const.tile([P, COMPONENTS], BF16)
         neg_mu = const.tile([P, COMPONENTS], F32)
         inv_mass = const.tile([P, COMPONENTS], F32)
 
+        def warm_up(count):
+            junk = ps_acc.tile([P, MX_COLUMNS], F32, name="acc")
+            for n in range(count):
+                nc.tensor.matmul(junk[:], lhsT=zeros[:, 0:P], rhs=zeros[:], start=True, stop=True)
+
         def prologue():
             load_z(0)
             nc.vector.memset(mu_rows[:], 0.0)
+            nc.vector.memset(zeros[:], 0.0)
             nc.scalar.dma_start(out=mu_rows[0:COMPONENTS, 0:DIM], in_=mu)
             nc.scalar.dma_start(out=mu_rows[0:COMPONENTS, DIM : 2 * DIM], in_=mu)
             nc.vector.memset(tick[:], 0.0)
@@ -95,6 +103,7 @@ def tile_gmmestimationnetwork_pa_kernel(tc, z_batch, gamma, mu, gamma_mass, out)
                 load_gamma(s)
             nc.sync.dma_start(out=mass_bf[:], in_=gamma_mass.partition_broadcast(P))
 
+            warm_up(WARM_AHEAD)
             mu_ps = ps_t.tile([P, P], BF16, tag="zt", name="mu_ps")
             nc.tensor.transpose(mu_ps[:], mu_rows[:], ident_bf[:])
             nc.vector.tensor_scalar_mul(out=neg_mu[:], in0=mu_ps[:, 0:COMPONENTS], scalar1=-1.0)
@@ -226,6 +235,8 @@ def tile_gmmestimationnetwork_pa_kernel(tc, z_batch, gamma, mu, gamma_mass, out)
             quantised[step] = (codes, scales)
 
         def multiply(step, half):
+            if step < 0:
+                warm_up(GROUP // 2)
             if not 0 <= step < STEPS:
                 return
             q, gg = divmod(step, GROUPS)

@@ -269,6 +269,7 @@ def tile_gmmestimationnetwork_pa_kernel(tc, z_batch, gamma, mu, gamma_mass, out)
             prologue()
             for i in range(-LEAD, STEPS + 2):
                 u0 = GROUP * i
+                transpose_z(i + LEAD)
                 multiply_gamma(u0 - 2)
                 fill(u0 + 4)
                 multiply(i - 2, 1)
@@ -280,7 +281,6 @@ def tile_gmmestimationnetwork_pa_kernel(tc, z_batch, gamma, mu, gamma_mass, out)
                 copy_zc(u0)
                 multiply_gamma(u0)
                 fill(u0 + 6)
-                transpose_z(i + LEAD)
                 quantise(i - 1)
                 multiply(i - 1, 0)
                 follow_vector(i)

@@ -27,9 +27,10 @@ Z_AHEAD = 8
 BANKS = 6
 SCALAR_BLOCKS = 5
 LEAD = 4
-GAMMA_PARTS = 4
-WARM_AHEAD = 3
-GAMMA_LEAD = 4
+GAMMA_PARTS = 8
+GAMMA_LEAD = 2
+WARM_AHEAD = 8
+WARM_FILL = 3
 MX_COLUMNS = 512
 
 FLOPS = 2 * COMPONENTS * SAMPLES * DIM * DIM
@@ -55,7 +56,7 @@ def tile_gmmestimationnetwork_pa_kernel(tc, z_batch, gamma, mu, gamma_mass, out)
             z_groups[gg] = zs
 
         gam_nat = const.tile([P, PASSES, PACK, COMPONENTS], BF16)
-        gam = const.tile([P, PASSES, COMPONENTS, PACK], BF16)
+        gam = [const.tile([P, PASSES, 2, PACK], BF16, name="gam%d" % q) for q in range(PAIRS)]
         part = PASSES // GAMMA_PARTS
 
         def load_gamma(s):
@@ -65,9 +66,9 @@ def tile_gmmestimationnetwork_pa_kernel(tc, z_batch, gamma, mu, gamma_mass, out)
                 in_=gamma_rows.rearrange("(g p j) c -> p g (j c)", p=P, j=PACK),
             )
 
-        def gamma_views(s):
+        def gamma_views(q, s):
             passes = slice(s * part, (s + 1) * part)
-            return gam[:, passes, :, :], gam_nat[:, passes, :, :].rearrange("p g j c -> p g c j")
+            return gam[q][:, passes, :, :], gam_nat[:, passes, :, 2 * q : 2 * q + 2].rearrange("p g j c -> p g c j")
 
         zT = const.tile([P, PASSES * 2, P], BF16)
         res = const.tile([P, PAIRS, DIM], F32)
@@ -90,37 +91,54 @@ def tile_gmmestimationnetwork_pa_kernel(tc, z_batch, gamma, mu, gamma_mass, out)
             load_z(0)
             nc.vector.memset(mu_rows[:], 0.0)
             nc.vector.memset(zeros[:], 0.0)
-            nc.scalar.dma_start(out=mu_rows[0:COMPONENTS, 0:DIM], in_=mu)
-            nc.scalar.dma_start(out=mu_rows[0:COMPONENTS, DIM : 2 * DIM], in_=mu)
+            nc.sync.dma_start(out=mu_rows[0:COMPONENTS, 0:DIM], in_=mu)
+            nc.sync.dma_start(out=mu_rows[0:COMPONENTS, DIM : 2 * DIM], in_=mu)
             nc.vector.memset(tick[:], 0.0)
             nc.scalar.activation(out=inv_mass[:, 0:1], in_=tick[:], func=ACTF.Identity, bias=0.0, scale=1.0)
             make_identity(nc, ident_bf[:])
             make_identity(nc, ident_f[:])
+            load_z(1)
+            load_z(2)
             load_gamma(0)
-            for gg in range(1, Z_AHEAD):
+            for gg in range(3, Z_AHEAD):
                 load_z(gg)
             for s in range(1, GAMMA_PARTS):
                 load_gamma(s)
             nc.sync.dma_start(out=mass_bf[:], in_=gamma_mass.partition_broadcast(P))
 
             warm_up(WARM_AHEAD)
-            mu_ps = ps_t.tile([P, P], BF16, tag="zt", name="mu_ps")
+            transpose_z(0)
+            mu_ps = ps_z.tile([P, P], BF16, tag="bank", name="mu_ps")
             nc.tensor.transpose(mu_ps[:], mu_rows[:], ident_bf[:])
             nc.vector.tensor_scalar_mul(out=neg_mu[:], in0=mu_ps[:, 0:COMPONENTS], scalar1=-1.0)
             nc.vector.tensor_copy(
                 out=perm_f[:].rearrange("k (d a) -> k d a", a=2), in_=ident_f[:].rearrange("k (a d) -> k d a", a=2)
             )
-            gam_part, nat_part = gamma_views(0)
+            for gg in range(1, LEAD):
+                transpose_z(gg, ps_z.tile([P, BLOCKS, P], BF16, tag="bank", name="zt_ahead"))
+            for gg in range(LEAD):
+                evacuate_z(gg)
+            for step in range(2):
+                for c2 in range(2):
+                    centre_vector(step, c2)
+            warm_up(WARM_FILL)
+            for u in range(GROUP):
+                fill(u)
+            gam_part, nat_part = gamma_views(0, 0)
             nc.vector.tensor_copy(out=gam_part, in_=nat_part)
+            nc.gpsimd.tensor_copy(out=tick[:], in_=centred[(1, 1)][:, BLOCKS - 1, P - 1 : P])
+            centre_second(2)
 
         def regroup_gamma(step):
-            s, ahead = divmod(step + GAMMA_LEAD, part // GROUP)
-            if not (1 <= s < GAMMA_PARTS and ahead == 0):
+            q, first = divmod(step + GAMMA_LEAD, GROUPS)
+            s, ahead = divmod(first, part // GROUP)
+            if ahead != 0 or q >= PAIRS or (q == 0 and s == 0):
                 return
-            gam_part, nat_part = gamma_views(s)
-            nc.gpsimd.tensor_scalar(
-                out=gam_part, in0=nat_part, scalar1=1.0, scalar2=0.0, op0=ALU.mult, op1=ALU.add
-            )
+            gam_part, nat_part = gamma_views(q, s)
+            if q == 0:
+                nc.vector.tensor_copy(out=gam_part, in_=nat_part)
+            else:
+                nc.gpsimd.tensor_scalar(out=gam_part, in0=nat_part, scalar1=1.0, scalar2=0.0, op0=ALU.mult, op1=ALU.add)
 
         zt_banks = {}
         centred = {}
@@ -129,11 +147,12 @@ def tile_gmmestimationnetwork_pa_kernel(tc, z_batch, gamma, mu, gamma_mass, out)
         quantised = {}
         accs = {}
 
-        def transpose_z(gg):
+        def transpose_z(gg, zt_ps=None):
             if not 0 <= gg < GROUPS:
                 return
             zs = z_groups[gg]
-            zt_ps = ps_t.tile([P, BLOCKS, P], BF16, tag="zt")
+            if zt_ps is None:
+                zt_ps = ps_t.tile([P, BLOCKS, P], BF16, name="zt")
             for b in range(BLOCKS):
                 g4, jj = divmod(b, 2)
                 nc.tensor.transpose(zt_ps[:, b, :], zs[:, g4, jj * P : (jj + 1) * P], ident_bf[:])
@@ -152,6 +171,13 @@ def tile_gmmestimationnetwork_pa_kernel(tc, z_batch, gamma, mu, gamma_mass, out)
             nc.gpsimd.tensor_scalar(
                 out=zc[:, first_block:BLOCKS, :], in0=zT[:, b0 + first_block : b0 + BLOCKS, :], scalar1=1.0,
                 scalar2=neg_mu[:, 2 * q + c2 : 2 * q + c2 + 1], op0=ALU.mult, op1=ALU.add,
+            )
+
+        def centre_vector(step, c2):
+            zc = (late if c2 else work).tile([P, BLOCKS, P], F32, name="zc%d" % c2)
+            centred[(step, c2)] = zc
+            nc.vector.tensor_scalar_add(
+                out=zc[:], in0=zT[:, step * BLOCKS : (step + 1) * BLOCKS, :], scalar1=neg_mu[:, c2 : c2 + 1]
             )
 
         def centre_second(step):
@@ -192,15 +218,11 @@ def tile_gmmestimationnetwork_pa_kernel(tc, z_batch, gamma, mu, gamma_mass, out)
             if not 0 <= u < UNITS:
                 return
             step, g4 = divmod(u, GROUP)
-            bank = ps_z.tile([P, 2, DIM, PACK], F32, name="bank")
+            bank = ps_z.tile([P, 2, 2, 2 * DIM], F32, name="bank")
             for c2 in range(2):
                 for jj in range(2):
-                    nc.tensor.transpose(
-                        bank[:, c2, :, 2 * jj : 2 * jj + 2],
-                        centred[(step, c2)][:, 2 * g4 + jj, :],
-                        perm_f[:],
-                    )
-            banks[u] = bank
+                    nc.tensor.transpose(bank[:, jj, c2, :], centred[(step, c2)][:, 2 * g4 + jj, :], perm_f[:])
+            banks[u] = bank[:].rearrange("p a c (d b) -> p c d a b", b=2)
 
         def copy_zc(u):
             if not 0 <= u < UNITS:
@@ -208,7 +230,9 @@ def tile_gmmestimationnetwork_pa_kernel(tc, z_batch, gamma, mu, gamma_mass, out)
             step, g4 = divmod(u, GROUP)
             if g4 == 0:
                 qins[step] = work.tile([P, 2, GROUP, WIDTH], BF16, name="qin", align_bytes=64)
-            nc.scalar.copy(out=qins[step][:, 0, g4, :], in_=banks[u][:].rearrange("p c d j -> p (c d j)"))
+            nc.scalar.copy(
+                out=qins[step][:, 0, g4, :].rearrange("p (c d a b) -> p c d a b", c=2, a=2, b=2), in_=banks[u]
+            )
 
         def multiply_gamma(u):
             if not 0 <= u < UNITS:
@@ -217,9 +241,9 @@ def tile_gmmestimationnetwork_pa_kernel(tc, z_batch, gamma, mu, gamma_mass, out)
             q, gg = divmod(step, GROUPS)
             g = gg * GROUP + g4
             nc.vector.tensor_tensor(
-                out=qins[step][:, 1, g4, :].rearrange("p (c d j) -> p c d j", c=2, j=PACK),
-                in0=banks[u][:],
-                in1=gam[:, g, 2 * q : 2 * q + 2, :].unsqueeze(2).to_broadcast([P, 2, DIM, PACK]),
+                out=qins[step][:, 1, g4, :].rearrange("p (c d a b) -> p c d a b", c=2, a=2, b=2),
+                in0=banks[u],
+                in1=gam[q][:, g, :, :].rearrange("p c (a b) -> p c a b", b=2).unsqueeze(2).to_broadcast([P, 2, DIM, 2, 2]),
                 op=ALU.mult,
             )
 
@@ -264,24 +288,31 @@ def tile_gmmestimationnetwork_pa_kernel(tc, z_batch, gamma, mu, gamma_mass, out)
                     out=res[own, q, :], in0=accs[q][own, own],
                     scalar1=inv_mass[own, 2 * q + c2 : 2 * q + c2 + 1],
                 )
+            if q >= PAIRS - 2:
+                store(0 if q == PAIRS - 2 else q, q + 1)
+
+        def store(first, end):
+            nc.sync.dma_start(
+                out=out[2 * first : 2 * end, :, :].rearrange("(q c) i j -> (c i) q j", c=2), in_=res[:, first:end, :]
+            )
 
         with tc.manual_schedule():
             prologue()
-            for i in range(-LEAD, STEPS + 2):
+            for i in range(STEPS + 2):
                 u0 = GROUP * i
                 transpose_z(i + LEAD)
                 multiply_gamma(u0 - 2)
                 fill(u0 + 4)
                 multiply(i - 2, 1)
                 multiply_gamma(u0 - 1)
-                if i == GAMMA_LEAD:
+                if i == LEAD:
                     nc.vector.reciprocal(out=inv_mass[:], in_=mass_bf[:])
-                finish(i - 2)
                 fill(u0 + 5)
                 copy_zc(u0)
                 multiply_gamma(u0)
                 fill(u0 + 6)
                 quantise(i - 1)
+                finish(i - 2)
                 multiply(i - 1, 0)
                 follow_vector(i)
                 centre_second(i + 3)
@@ -294,5 +325,3 @@ def tile_gmmestimationnetwork_pa_kernel(tc, z_batch, gamma, mu, gamma_mass, out)
                 copy_zc(u0 + 3)
                 centre_first_scalar(i + 2)
                 evacuate_z(i + LEAD)
-
-        nc.sync.dma_start(out=out.rearrange("(q c) i j -> (c i) q j", c=2), in_=res[:])

@@ -25,7 +25,9 @@ BLOCKS = 2 * GROUP
 WIDTH = 2 * DIM * PACK
 Z_AHEAD = 8
 BANKS = 6
-SCALAR_BLOCKS = 5
+CENTRE_SPLIT = ((5, 8), (8, 8), (5, 5), (5, 5))
+SHARE_FROM = 2
+SHARED_PASS, SHARED_C2 = 0, 1
 LEAD = 4
 GAMMA_PARTS = 8
 GAMMA_LEAD = 2
@@ -81,6 +83,9 @@ def tile_gmmestimationnetwork_pa_kernel(tc, z_batch, gamma, mu, gamma_mass, out)
         mass_bf = const.tile([P, COMPONENTS], BF16)
         neg_mu = const.tile([P, COMPONENTS], F32)
         inv_mass = const.tile([P, COMPONENTS], F32)
+        gam_shared = const.tile([P, PAIRS - SHARE_FROM, GROUPS, PACK], F32)
+        first_wide = CENTRE_SPLIT[SHARE_FROM][1]
+        zT_wide = const.tile([P, GROUPS, BLOCKS - first_wide, P], F32)
 
         def warm_up(count):
             junk = ps_acc.tile([P, MX_COLUMNS], F32, name="acc")
@@ -140,9 +145,29 @@ def tile_gmmestimationnetwork_pa_kernel(tc, z_batch, gamma, mu, gamma_mass, out)
             else:
                 nc.gpsimd.tensor_scalar(out=gam_part, in0=nat_part, scalar1=1.0, scalar2=0.0, op0=ALU.mult, op1=ALU.add)
 
+        def widen_gamma():
+            for q in range(SHARE_FROM, PAIRS):
+                nc.vector.tensor_copy(
+                    out=gam_shared[:, q - SHARE_FROM, :, :], in_=gam_nat[:, SHARED_PASS::GROUP, :, 2 * q + SHARED_C2]
+                )
+
+        def widen_z(step):
+            q, gg = divmod(step, GROUPS)
+            if q != SHARE_FROM - 1:
+                return
+            nc.gpsimd.tensor_scalar(
+                out=zT_wide[:, gg, :, :], in0=zT[:, gg * BLOCKS + first_wide : (gg + 1) * BLOCKS, :],
+                scalar1=1.0, scalar2=0.0, op0=ALU.mult, op1=ALU.add,
+            )
+
+        def shared(u):
+            step, g4 = divmod(u, GROUP)
+            return step >= SHARE_FROM * GROUPS and g4 == SHARED_PASS
+
         zt_banks = {}
         centred = {}
         banks = {}
+        shared_rows = {}
         qins = {}
         quantised = {}
         accs = {}
@@ -165,11 +190,11 @@ def tile_gmmestimationnetwork_pa_kernel(tc, z_batch, gamma, mu, gamma_mass, out)
             if gg + Z_AHEAD < GROUPS:
                 load_z(gg + Z_AHEAD)
 
-        def centre_gpsimd(zc, step, c2, first_block):
+        def centre_gpsimd(zc, step, c2, first, end):
             q, gg = divmod(step, GROUPS)
             b0 = gg * BLOCKS
             nc.gpsimd.tensor_scalar(
-                out=zc[:, first_block:BLOCKS, :], in0=zT[:, b0 + first_block : b0 + BLOCKS, :], scalar1=1.0,
+                out=zc[:, first:end, :], in0=zT[:, b0 + first : b0 + end, :], scalar1=1.0,
                 scalar2=neg_mu[:, 2 * q + c2 : 2 * q + c2 + 1], op0=ALU.mult, op1=ALU.add,
             )
 
@@ -185,25 +210,23 @@ def tile_gmmestimationnetwork_pa_kernel(tc, z_batch, gamma, mu, gamma_mass, out)
                 return
             zc1 = late.tile([P, BLOCKS, P], F32, name="zc1")
             centred[(step, 1)] = zc1
-            centre_gpsimd(zc1, step, 1, 0)
-
-        def scalar_blocks(step):
-            return SCALAR_BLOCKS if step < GROUPS else BLOCKS
+            centre_gpsimd(zc1, step, 1, 0, BLOCKS)
 
         def centre_first_gpsimd(step):
             if not 0 <= step < STEPS:
                 return
             zc0 = work.tile([P, BLOCKS, P], F32, name="zc0")
             centred[(step, 0)] = zc0
-            if scalar_blocks(step) < BLOCKS:
-                centre_gpsimd(zc0, step, 0, scalar_blocks(step))
+            first, end = CENTRE_SPLIT[step // GROUPS]
+            if first < end:
+                centre_gpsimd(zc0, step, 0, first, end)
 
         def centre_first_scalar(step):
             if not 0 <= step < STEPS:
                 return
             q, gg = divmod(step, GROUPS)
             b0 = gg * BLOCKS
-            blocks = scalar_blocks(step)
+            blocks = CENTRE_SPLIT[q][0]
             nc.scalar.activation(
                 out=centred[(step, 0)][:, 0:blocks, :], in_=zT[:, b0 : b0 + blocks, :],
                 func=ACTF.Identity, bias=neg_mu[:, 2 * q : 2 * q + 1], scale=1.0,
@@ -219,9 +242,18 @@ def tile_gmmestimationnetwork_pa_kernel(tc, z_batch, gamma, mu, gamma_mass, out)
                 return
             step, g4 = divmod(u, GROUP)
             bank = ps_z.tile([P, 2, 2, 2 * DIM], F32, name="bank")
+            q, gg = divmod(step, GROUPS)
             for c2 in range(2):
                 for jj in range(2):
-                    nc.tensor.transpose(bank[:, jj, c2, :], centred[(step, c2)][:, 2 * g4 + jj, :], perm_f[:])
+                    b = 2 * g4 + jj
+                    if c2 == 0 and b >= CENTRE_SPLIT[q][1]:
+                        shift = neg_mu[:, 2 * q : 2 * q + 1].to_broadcast([P, P])
+                        for n, lhsT in enumerate((shift, zT_wide[:, gg, b - first_wide, :])):
+                            nc.tensor.matmul(
+                                bank[:, jj, c2, :], lhsT=lhsT, rhs=perm_f[:], start=(n == 0), stop=(n == 1), is_transpose=True
+                            )
+                    else:
+                        nc.tensor.transpose(bank[:, jj, c2, :], centred[(step, c2)][:, b, :], perm_f[:])
             banks[u] = bank[:].rearrange("p a c (d b) -> p c d a b", b=2)
 
         def copy_zc(u):
@@ -234,16 +266,41 @@ def tile_gmmestimationnetwork_pa_kernel(tc, z_batch, gamma, mu, gamma_mass, out)
                 out=qins[step][:, 0, g4, :].rearrange("p (c d a b) -> p c d a b", c=2, a=2, b=2), in_=banks[u]
             )
 
+        def scale_shared(u):
+            if not (0 <= u < UNITS and shared(u)):
+                return
+            q, gg = divmod(u // GROUP, GROUPS)
+            gz_rows = work.tile([P, PACK, DIM], BF16, name="gz_rows")
+            for j in range(PACK):
+                nc.scalar.activation(
+                    out=gz_rows[:, j, :], in_=banks[u][:, SHARED_C2, :, j // 2, j % 2],
+                    func=ACTF.Copy, bias=0.0, scale=gam_shared[:, q - SHARE_FROM, gg, j : j + 1],
+                )
+            shared_rows[u] = gz_rows
+
+        def interleave_shared(u):
+            if not (0 <= u < UNITS and shared(u)):
+                return
+            step, g4 = divmod(u, GROUP)
+            cols = slice(SHARED_C2 * DIM * PACK, (SHARED_C2 + 1) * DIM * PACK)
+            nc.gpsimd.tensor_scalar(
+                out=qins[step][:, 1, g4, cols].rearrange("p (d j) -> p d j", j=PACK),
+                in0=shared_rows[u][:].rearrange("p j d -> p d j"),
+                scalar1=1.0, scalar2=0.0, op0=ALU.mult, op1=ALU.add,
+            )
+
         def multiply_gamma(u):
             if not 0 <= u < UNITS:
                 return
             step, g4 = divmod(u, GROUP)
             q, gg = divmod(step, GROUPS)
             g = gg * GROUP + g4
+            n = SHARED_C2 if shared(u) else 2
+            factors = gam[q][:, g, 0:n, :].rearrange("p c (a b) -> p c a b", b=2)
             nc.vector.tensor_tensor(
-                out=qins[step][:, 1, g4, :].rearrange("p (c d a b) -> p c d a b", c=2, a=2, b=2),
-                in0=banks[u],
-                in1=gam[q][:, g, :, :].rearrange("p c (a b) -> p c a b", b=2).unsqueeze(2).to_broadcast([P, 2, DIM, 2, 2]),
+                out=qins[step][:, 1, g4, 0 : n * DIM * PACK].rearrange("p (c d a b) -> p c d a b", c=n, a=2, b=2),
+                in0=banks[u][:, 0:n, :, :, :],
+                in1=factors.unsqueeze(2).to_broadcast([P, n, DIM, 2, 2]),
                 op=ALU.mult,
             )
 
@@ -309,15 +366,20 @@ def tile_gmmestimationnetwork_pa_kernel(tc, z_batch, gamma, mu, gamma_mass, out)
                     nc.vector.reciprocal(out=inv_mass[:], in_=mass_bf[:])
                 fill(u0 + 5)
                 copy_zc(u0)
+                scale_shared(u0)
                 multiply_gamma(u0)
                 fill(u0 + 6)
                 quantise(i - 1)
                 finish(i - 2)
                 multiply(i - 1, 0)
                 follow_vector(i)
+                interleave_shared(u0)
                 centre_second(i + 3)
                 centre_first_gpsimd(i + 2)
                 regroup_gamma(i)
+                widen_z(i)
+                if i == GROUPS:
+                    widen_gamma()
                 copy_zc(u0 + 1)
                 multiply_gamma(u0 + 1)
                 fill(u0 + 7)

@@ -26,6 +26,7 @@ WIDTH = 2 * DIM * PACK
 Z_AHEAD = 8
 BANKS = 6
 CENTRE_SPLIT = ((5, 8), (8, 8), (5, 5), (5, 5))
+SECOND_SPLIT = (8, 8, 7, 7)
 SHARE_FROM = 2
 SHARED_PASS, SHARED_C2 = 0, 1
 LEAD = 4
@@ -210,7 +211,7 @@ def tile_gmmestimationnetwork_pa_kernel(tc, z_batch, gamma, mu, gamma_mass, out)
                 return
             zc1 = late.tile([P, BLOCKS, P], F32, name="zc1")
             centred[(step, 1)] = zc1
-            centre_gpsimd(zc1, step, 1, 0, BLOCKS)
+            centre_gpsimd(zc1, step, 1, 0, SECOND_SPLIT[step // GROUPS])
 
         def centre_first_gpsimd(step):
             if not 0 <= step < STEPS:
@@ -246,8 +247,8 @@ def tile_gmmestimationnetwork_pa_kernel(tc, z_batch, gamma, mu, gamma_mass, out)
             for c2 in range(2):
                 for jj in range(2):
                     b = 2 * g4 + jj
-                    if c2 == 0 and b >= CENTRE_SPLIT[q][1]:
-                        shift = neg_mu[:, 2 * q : 2 * q + 1].to_broadcast([P, P])
+                    if b >= (CENTRE_SPLIT[q][1], SECOND_SPLIT[q])[c2]:
+                        shift = neg_mu[:, 2 * q + c2 : 2 * q + c2 + 1].to_broadcast([P, P])
                         for n, lhsT in enumerate((shift, zT_wide[:, gg, b - first_wide, :])):
                             nc.tensor.matmul(
                                 bank[:, jj, c2, :], lhsT=lhsT, rhs=perm_f[:], start=(n == 0), stop=(n == 1), is_transpose=True

@@ -26,7 +26,7 @@ WIDTH = 2 * DIM * PACK
 Z_AHEAD = 8
 BANKS = 6
 CENTRE_SPLIT = ((5, 8), (8, 8), (5, 5), (5, 5))
-SECOND_SPLIT = (8, 8, 7, 7)
+SECOND_SPLIT = (8, 6, 7, 7)
 SHARE_FROM = 2
 SHARED_PASS, SHARED_C2 = 0, 1
 LEAD = 4
@@ -375,10 +375,10 @@ def tile_gmmestimationnetwork_pa_kernel(tc, z_batch, gamma, mu, gamma_mass, out)
                 multiply(i - 1, 0)
                 follow_vector(i)
                 interleave_shared(u0)
+                widen_z(i + 3)
                 centre_second(i + 3)
                 centre_first_gpsimd(i + 2)
                 regroup_gamma(i)
-                widen_z(i)
                 if i == GROUPS:
                     widen_gamma()
                 copy_zc(u0 + 1)

from contextlib import ExitStack

import concourse.mybir as mybir
from concourse.masks import make_identity

F32 = mybir.dt.float32
BF16 = mybir.dt.bfloat16
U32 = mybir.dt.uint32
U8 = mybir.dt.uint8
FP8X4 = mybir.dt.float8_e4m3fn_x4
ALU = mybir.AluOpType
ACTF = mybir.ActivationFunctionType

SAMPLES, DIM, COMPONENTS = 65536, 64, 8
P = 128
PACK = 4
K_PASS = P * PACK
PASSES = SAMPLES // K_PASS
GROUP = 4
GROUPS = PASSES // GROUP
PAIRS = COMPONENTS // 2
STEPS = PAIRS * GROUPS
UNITS = STEPS * GROUP
BLOCKS = 2 * GROUP
WIDTH = 2 * DIM * PACK
Z_AHEAD = 8
BANKS = 6
CENTRE_SPLIT = ((5, 8), (8, 8), (5, 5), (5, 5))
SECOND_SPLIT = (8, 6, 7, 7)
SHARE_FROM = 2
SHARED_PASS, SHARED_C2 = 0, 1
LEAD = 4
GAMMA_PARTS = 8
GAMMA_LEAD = 2
WARM_AHEAD = 8
WARM_FILL = 3
MX_COLUMNS = 512

FLOPS = 2 * COMPONENTS * SAMPLES * DIM * DIM


def tile_gmmestimationnetwork_pa_kernel(tc, z_batch, gamma, mu, gamma_mass, out):
    nc = tc.nc
    with ExitStack() as ctx:
        const = ctx.enter_context(tc.tile_pool(name="const", bufs=1))
        stage = ctx.enter_context(tc.tile_pool(name="stage", bufs=Z_AHEAD))
        work = ctx.enter_context(tc.tile_pool(name="work", bufs=3))
        late = ctx.enter_context(tc.tile_pool(name="late", bufs=4))
        ps_t = ctx.enter_context(tc.psum_pool(name="ps_t", bufs=1))
        ps_z = ctx.enter_context(tc.psum_pool(name="ps_z", bufs=BANKS))
        ps_acc = ctx.enter_context(tc.psum_pool(name="ps_acc", bufs=1))

        z_groups = {}

        def load_z(gg):
            zs = stage.tile([P, GROUP, PACK * DIM], BF16, name="zs")
            z_rows = z_batch[gg * GROUP * K_PASS : (gg + 1) * GROUP * K_PASS, :]
            nc.sync.dma_start(out=zs[:], in_=z_rows.rearrange("(g p j) d -> p g (j d)", p=P, j=PACK))
            z_groups[gg] = zs

        gam_nat = const.tile([P, PASSES, PACK, COMPONENTS], BF16)
        gam = [const.tile([P, PASSES, 2, PACK], BF16, name="gam%d" % q) for q in range(PAIRS)]
        part = PASSES // GAMMA_PARTS

        def load_gamma(s):
            gamma_rows = gamma[s * part * K_PASS : (s + 1) * part * K_PASS, :]
            nc.sync.dma_start(
                out=gam_nat[:, s * part : (s + 1) * part, :, :].rearrange("p g j c -> p g (j c)"),
                in_=gamma_rows.rearrange("(g p j) c -> p g (j c)", p=P, j=PACK),
            )

        def gamma_views(q, s):
            passes = slice(s * part, (s + 1) * part)
            return gam[q][:, passes, :, :], gam_nat[:, passes, :, 2 * q : 2 * q + 2].rearrange("p g j c -> p g c j")

        zT = const.tile([P, PASSES * 2, P], BF16)
        res = const.tile([P, PAIRS, DIM], F32)
        tick = const.tile([P, 1], BF16)
        ident_bf = const.tile([P, P], BF16)
        ident_f = const.tile([P, P], F32)
        perm_f = const.tile([P, P], F32)
        mu_rows = const.tile([P, P], BF16)
        zeros = const.tile([P, MX_COLUMNS], BF16)
        mass_bf = const.tile([P, COMPONENTS], BF16)
        neg_mu = const.tile([P, COMPONENTS], F32)
        inv_mass = const.tile([P, COMPONENTS], F32)
        gam_shared = const.tile([P, PAIRS - SHARE_FROM, GROUPS, PACK], F32)
        first_wide = CENTRE_SPLIT[SHARE_FROM][1]
        zT_wide = const.tile([P, GROUPS, BLOCKS - first_wide, P], F32)

        def warm_up(count):
            junk = ps_acc.tile([P, MX_COLUMNS], F32, name="acc")
            for n in range(count):
                nc.tensor.matmul(junk[:], lhsT=zeros[:, 0:P], rhs=zeros[:], start=True, stop=True)

        def prologue():
            load_z(0)
            nc.vector.memset(mu_rows[:], 0.0)
            nc.vector.memset(zeros[:], 0.0)
            nc.sync.dma_start(out=mu_rows[0:COMPONENTS, 0:DIM], in_=mu)
            nc.sync.dma_start(out=mu_rows[0:COMPONENTS, DIM : 2 * DIM], in_=mu)
            nc.vector.memset(tick[:], 0.0)
            nc.scalar.activation(out=inv_mass[:, 0:1], in_=tick[:], func=ACTF.Identity, bias=0.0, scale=1.0)
            make_identity(nc, ident_bf[:])
            make_identity(nc, ident_f[:])
            load_z(1)
            load_z(2)
            load_gamma(0)
            for gg in range(3, Z_AHEAD):
                load_z(gg)
            for s in range(1, GAMMA_PARTS):
                load_gamma(s)
            nc.sync.dma_start(out=mass_bf[:], in_=gamma_mass.partition_broadcast(P))

            warm_up(WARM_AHEAD)
            transpose_z(0)
            mu_ps = ps_z.tile([P, P], BF16, tag="bank", name="mu_ps")
            nc.tensor.transpose(mu_ps[:], mu_rows[:], ident_bf[:])
            nc.vector.tensor_scalar_mul(out=neg_mu[:], in0=mu_ps[:, 0:COMPONENTS], scalar1=-1.0)
            nc.vector.tensor_copy(
                out=perm_f[:].rearrange("k (d a) -> k d a", a=2), in_=ident_f[:].rearrange("k (a d) -> k d a", a=2)
            )
            for gg in range(1, LEAD):
                transpose_z(gg, ps_z.tile([P, BLOCKS, P], BF16, tag="bank", name="zt_ahead"))
            for gg in range(LEAD):
                evacuate_z(gg)
            for step in range(2):
                for c2 in range(2):
                    centre_vector(step, c2)
            warm_up(WARM_FILL)
            for u in range(GROUP):
                fill(u)
            gam_part, nat_part = gamma_views(0, 0)
            nc.vector.tensor_copy(out=gam_part, in_=nat_part)
            nc.gpsimd.tensor_copy(out=tick[:], in_=centred[(1, 1)][:, BLOCKS - 1, P - 1 : P])
            centre_second(2)

        def regroup_gamma(step):
            q, first = divmod(step + GAMMA_LEAD, GROUPS)
            s, ahead = divmod(first, part // GROUP)
            if ahead != 0 or q >= PAIRS or (q == 0 and s == 0):
                return
            gam_part, nat_part = gamma_views(q, s)
            if q == 0:
                nc.vector.tensor_copy(out=gam_part, in_=nat_part)
            else:
                nc.gpsimd.tensor_scalar(out=gam_part, in0=nat_part, scalar1=1.0, scalar2=0.0, op0=ALU.mult, op1=ALU.add)

        def widen_gamma():
            for q in range(SHARE_FROM, PAIRS):
                nc.vector.tensor_copy(
                    out=gam_shared[:, q - SHARE_FROM, :, :], in_=gam_nat[:, SHARED_PASS::GROUP, :, 2 * q + SHARED_C2]
                )

        def widen_z(step):
            q, gg = divmod(step, GROUPS)
            if q != SHARE_FROM - 1:
                return
            nc.gpsimd.tensor_scalar(
                out=zT_wide[:, gg, :, :], in0=zT[:, gg * BLOCKS + first_wide : (gg + 1) * BLOCKS, :],
                scalar1=1.0, scalar2=0.0, op0=ALU.mult, op1=ALU.add,
            )

        def shared(u):
            step, g4 = divmod(u, GROUP)
            return step >= SHARE_FROM * GROUPS and g4 == SHARED_PASS

        zt_banks = {}
        centred = {}
        banks = {}
        shared_rows = {}
        qins = {}
        quantised = {}
        accs = {}

        def transpose_z(gg, zt_ps=None):
            if not 0 <= gg < GROUPS:
                return
            zs = z_groups[gg]
            if zt_ps is None:
                zt_ps = ps_t.tile([P, BLOCKS, P], BF16, name="zt")
            for b in range(BLOCKS):
                g4, jj = divmod(b, 2)
                nc.tensor.transpose(zt_ps[:, b, :], zs[:, g4, jj * P : (jj + 1) * P], ident_bf[:])
            zt_banks[gg] = zt_ps

        def evacuate_z(gg):
            if not 0 <= gg < GROUPS:
                return
            nc.scalar.copy(out=zT[:, gg * BLOCKS : (gg + 1) * BLOCKS, :], in_=zt_banks[gg][:])
            if gg + Z_AHEAD < GROUPS:
                load_z(gg + Z_AHEAD)

        def centre_gpsimd(zc, step, c2, first, end):
            q, gg = divmod(step, GROUPS)
            b0 = gg * BLOCKS
            nc.gpsimd.tensor_scalar(
                out=zc[:, first:end, :], in0=zT[:, b0 + first : b0 + end, :], scalar1=1.0,
                scalar2=neg_mu[:, 2 * q + c2 : 2 * q + c2 + 1], op0=ALU.mult, op1=ALU.add,
            )

        def centre_vector(step, c2):
            zc = (late if c2 else work).tile([P, BLOCKS, P], F32, name="zc%d" % c2)
            centred[(step, c2)] = zc
            nc.vector.tensor_scalar_add(
                out=zc[:], in0=zT[:, step * BLOCKS : (step + 1) * BLOCKS, :], scalar1=neg_mu[:, c2 : c2 + 1]
            )

        def centre_second(step):
            if not 0 <= step < STEPS:
                return
            zc1 = late.tile([P, BLOCKS, P], F32, name="zc1")
            centred[(step, 1)] = zc1
            centre_gpsimd(zc1, step, 1, 0, SECOND_SPLIT[step // GROUPS])

        def centre_first_gpsimd(step):
            if not 0 <= step < STEPS:
                return
            zc0 = work.tile([P, BLOCKS, P], F32, name="zc0")
            centred[(step, 0)] = zc0
            first, end = CENTRE_SPLIT[step // GROUPS]
            if first < end:
                centre_gpsimd(zc0, step, 0, first, end)

        def centre_first_scalar(step):
            if not 0 <= step < STEPS:
                return
            q, gg = divmod(step, GROUPS)
            b0 = gg * BLOCKS
            blocks = CENTRE_SPLIT[q][0]
            nc.scalar.activation(
                out=centred[(step, 0)][:, 0:blocks, :], in_=zT[:, b0 : b0 + blocks, :],
                func=ACTF.Identity, bias=neg_mu[:, 2 * q : 2 * q + 1], scale=1.0,
            )

        def follow_vector(step):
            if not 0 <= step < STEPS - 3:
                return
            nc.gpsimd.tensor_copy(out=tick[:], in_=qins[step][:, 1, 0, 0:1])

        def fill(u):
            if not 0 <= u < UNITS:
                return
            step, g4 = divmod(u, GROUP)
            bank = ps_z.tile([P, 2, 2, 2 * DIM], F32, name="bank")
            q, gg = divmod(step, GROUPS)
            for c2 in range(2):
                for jj in range(2):
                    b = 2 * g4 + jj
                    if b >= (CENTRE_SPLIT[q][1], SECOND_SPLIT[q])[c2]:
                        shift = neg_mu[:, 2 * q + c2 : 2 * q + c2 + 1].to_broadcast([P, P])
                        for n, lhsT in enumerate((shift, zT_wide[:, gg, b - first_wide, :])):
                            nc.tensor.matmul(
                                bank[:, jj, c2, :], lhsT=lhsT, rhs=perm_f[:], start=(n == 0), stop=(n == 1), is_transpose=True
                            )
                    else:
                        nc.tensor.transpose(bank[:, jj, c2, :], centred[(step, c2)][:, b, :], perm_f[:])
            banks[u] = bank[:].rearrange("p a c (d b) -> p c d a b", b=2)

        def copy_zc(u):
            if not 0 <= u < UNITS:
                return
            step, g4 = divmod(u, GROUP)
            if g4 == 0:
                qins[step] = work.tile([P, 2, GROUP, WIDTH], BF16, name="qin", align_bytes=64)
            nc.scalar.copy(
                out=qins[step][:, 0, g4, :].rearrange("p (c d a b) -> p c d a b", c=2, a=2, b=2), in_=banks[u]
            )

        def scale_shared(u):
            if not (0 <= u < UNITS and shared(u)):
                return
            q, gg = divmod(u // GROUP, GROUPS)
            gz_rows = work.tile([P, PACK, DIM], BF16, name="gz_rows")
            for j in range(PACK):
                nc.scalar.activation(
                    out=gz_rows[:, j, :], in_=banks[u][:, SHARED_C2, :, j // 2, j % 2],
                    func=ACTF.Copy, bias=0.0, scale=gam_shared[:, q - SHARE_FROM, gg, j : j + 1],
                )
            shared_rows[u] = gz_rows

        def interleave_shared(u):
            if not (0 <= u < UNITS and shared(u)):
                return
            step, g4 = divmod(u, GROUP)
            cols = slice(SHARED_C2 * DIM * PACK, (SHARED_C2 + 1) * DIM * PACK)
            nc.gpsimd.tensor_scalar(
                out=qins[step][:, 1, g4, cols].rearrange("p (d j) -> p d j", j=PACK),
                in0=shared_rows[u][:].rearrange("p j d -> p d j"),
                scalar1=1.0, scalar2=0.0, op0=ALU.mult, op1=ALU.add,
            )

        def multiply_gamma(u):
            if not 0 <= u < UNITS:
                return
            step, g4 = divmod(u, GROUP)
            q, gg = divmod(step, GROUPS)
            g = gg * GROUP + g4
            n = SHARED_C2 if shared(u) else 2
            factors = gam[q][:, g, 0:n, :].rearrange("p c (a b) -> p c a b", b=2)
            nc.vector.tensor_tensor(
                out=qins[step][:, 1, g4, 0 : n * DIM * PACK].rearrange("p (c d a b) -> p c d a b", c=n, a=2, b=2),
                in0=banks[u][:, 0:n, :, :, :],
                in1=factors.unsqueeze(2).to_broadcast([P, n, DIM, 2, 2]),
                op=ALU.mult,
            )

        def quantise(step):
            if not 0 <= step < STEPS:
                return
            codes = work.tile([P, 2 * GROUP * P], U32, name="codes", align_bytes=64)
            scales = work.tile([P, 2 * GROUP * P], U8, name="scales", align_bytes=64)
            nc.vector.quantize_mx(
                out=codes[:].bitcast(FP8X4), scales=scales[:],
                in_=qins[step][:].rearrange("p a g w -> p (a g w)"),
            )
            quantised[step] = (codes, scales)

        def multiply(step, half):
            if step < 0:
                warm_up(GROUP // 2)
            if not 0 <= step < STEPS:
                return
            q, gg = divmod(step, GROUPS)
            codes, scales = quantised[step]
            if gg == 0 and half == 0:
                accs[q] = ps_acc.tile([P, MX_COLUMNS], F32, name="acc")
            for g4 in range(2 * half, 2 * half + 2):
                g = gg * GROUP + g4
                zc_cols = slice(g4 * P, g4 * P + MX_COLUMNS)
                gz_cols = slice((GROUP + g4) * P, (GROUP + g4 + 1) * P)
                nc.tensor.matmul_mx(
                    out=accs[q][:],
                    lhsT=codes[:, gz_cols].bitcast(FP8X4), lhsT_scale=scales[:, gz_cols],
                    rhs=codes[:, zc_cols].bitcast(FP8X4), rhs_scale=scales[:, zc_cols],
                    start=(g == 0), stop=(g == PASSES - 1),
                )

        def finish(step):
            q, gg = divmod(step, GROUPS)
            if not (0 <= step and gg == GROUPS - 1):
                return
            for c2 in range(2):
                own = slice(c2 * DIM, (c2 + 1) * DIM)
                nc.vector.tensor_scalar_mul(
                    out=res[own, q, :], in0=accs[q][own, own],
                    scalar1=inv_mass[own, 2 * q + c2 : 2 * q + c2 + 1],
                )
            if q >= PAIRS - 2:
                store(0 if q == PAIRS - 2 else q, q + 1)

        def store(first, end):
            nc.sync.dma_start(
                out=out[2 * first : 2 * end, :, :].rearrange("(q c) i j -> (c i) q j", c=2), in_=res[:, first:end, :]
            )

        with tc.manual_schedule():
            prologue()
            for i in range(STEPS + 2):
                u0 = GROUP * i
                transpose_z(i + LEAD)
                multiply_gamma(u0 - 2)
                fill(u0 + 4)
                multiply(i - 2, 1)
                multiply_gamma(u0 - 1)
                if i == LEAD:
                    nc.vector.reciprocal(out=inv_mass[:], in_=mass_bf[:])
                fill(u0 + 5)
                copy_zc(u0)
                scale_shared(u0)
                multiply_gamma(u0)
                fill(u0 + 6)
                quantise(i - 1)
                finish(i - 2)
                multiply(i - 1, 0)
                follow_vector(i)
                interleave_shared(u0)
                widen_z(i + 3)
                centre_second(i + 3)
                centre_first_gpsimd(i + 2)
                regroup_gamma(i)
                if i == GROUPS:
                    widen_gamma()
                copy_zc(u0 + 1)
                multiply_gamma(u0 + 1)
                fill(u0 + 7)
                copy_zc(u0 + 2)
                copy_zc(u0 + 3)
                centre_first_scalar(i + 2)
                evacuate_z(i + LEAD)
